import numpy as np
import ml_dtypes


def mxq(x, axis, fmt="e4m3"):
    dtype, down = {"e4m3": (ml_dtypes.float8_e4m3fn, 7), "e5m2": (ml_dtypes.float8_e5m2, 14)}[fmt]
    v = np.moveaxis(np.asarray(x, np.float32).astype(ml_dtypes.bfloat16).astype(np.float64), axis, -1)
    blocks = v.reshape(v.shape[:-1] + (-1, 32))
    amax = np.abs(blocks).max(-1, keepdims=True)
    byte = np.maximum(np.where(amax > 0, np.frexp(amax)[1] - 1 + 127, 0) - down, 1)
    scale = np.exp2(byte - 127.0)
    codes = (blocks / scale).astype(np.float32).astype(dtype).astype(np.float64)
    return np.moveaxis((codes * scale).reshape(v.shape), -1, axis)


WIDE = False


def mx_kscale(k):
    if not WIDE:
        return np.ones(k)
    levels = np.array([10, -10, 5, -5, 0])
    a = np.random.permutation(np.resize(levels, k // 512 * 4)).reshape(k // 512, 4)
    idx = np.arange(k)
    return np.exp2(a[idx // 512, idx % 128 // 32])


BF16 = ml_dtypes.bfloat16


def bf(x):
    return np.asarray(x, np.float32).astype(BF16)


def f64(x):
    return np.asarray(x).astype(np.float64)


E2M1 = np.array([0.0, 0.5, 1.0, 1.5, 2.0, 3.0, 4.0, 6.0, -0.0, -0.5, -1.0, -1.5, -2.0, -3.0, -4.0, -6.0])


def pack_weight(w, fmt):
    k, n = w.shape
    w = f64(bf(w)).reshape(k // 32, 32, n)
    amax = np.abs(w).max(1)
    if fmt == "e4m3":
        byte = np.frexp(amax)[1] - 1 + 127 - 7
    else:
        mant, ex = np.frexp(amax / 6.0)
        byte = np.where(mant > 0.5, ex, ex - 1) + 127
    byte = np.clip(np.where(amax > 0, byte, 1), 1, 254)
    scaled = (w * np.exp2(127.0 - byte)[:, None, :]).reshape(k, n).astype(np.float32)
    by_word = np.ascontiguousarray(scaled.reshape(k // 512, 128, 4, n).transpose(0, 1, 3, 2))
    if fmt == "e4m3":
        words = by_word.astype(ml_dtypes.float8_e4m3fn).view(np.uint8)
    else:
        c = by_word.astype(ml_dtypes.float4_e2m1fn).view(np.uint8) & 0xF
        words = c[..., 0::2] | (c[..., 1::2] << 4)
    return np.ascontiguousarray(words), np.ascontiguousarray(byte.astype(np.uint8).reshape(k // 512, 16, n))


def unpack_weight(words, scales, fmt):
    g, p, n, _ = words.shape
    if fmt == "e4m3":
        vals = np.ascontiguousarray(words).view(ml_dtypes.float8_e4m3fn).astype(np.float64)
    else:
        nib = np.empty((g, p, n, 4), np.uint8)
        nib[..., 0::2] = words & 0xF
        nib[..., 1::2] = words >> 4
        vals = E2M1[nib]
    vals = vals * np.repeat(np.exp2(scales.astype(np.float64) - 127.0), 8, axis=1)[..., None]
    return vals.transpose(0, 1, 3, 2).reshape(g * 512, n)


BATCH, SEQ, IN_F, OUT_F, GRID_SIZE = 4, 128, 1024, 1024, 8
GRID_LO, GRID_HI = -2.0, 2.0


def _grid_and_inv_denom():
    grid = np.linspace(GRID_LO, GRID_HI, GRID_SIZE)
    inv_denom = 1.0 / (float((GRID_HI - GRID_LO) / (GRID_SIZE - 1)) + 1e-06)
    return grid, inv_denom


def silu(v):
    e = np.exp(-np.abs(v))
    return v * np.where(v >= 0.0, 1.0, e) / (1.0 + e)


def setup_inputs():
    s = mx_kscale(IN_F)
    x = bf(np.random.standard_normal((BATCH, SEQ, IN_F)) * s)
    base_w = np.random.standard_normal((OUT_F, IN_F)) / np.sqrt(IN_F) / s
    base_w_words, base_w_scales = pack_weight(np.ascontiguousarray(base_w.T), "e4m3")
    base_b = bf(np.random.standard_normal(OUT_F) * 0.1)
    spline_w = bf(np.random.standard_normal((OUT_F, IN_F, GRID_SIZE)) * 0.64 / np.sqrt(IN_F))
    return {"x": x,
            "base_w_words": base_w_words,
            "base_w_scales": base_w_scales,
            "base_b": base_b,
            "spline_w": spline_w}


def reference(x, base_w_words, base_w_scales, base_b, spline_w):
    grid, inv_denom = _grid_and_inv_denom()
    lead = x.shape[:-1]
    x_flat = f64(x).reshape(-1, IN_F)
    act = silu(x_flat)
    base_out = (mxq(act, 1, "e4m3") @ unpack_weight(base_w_words, base_w_scales, "e4m3")) + f64(base_b)
    basis = np.exp(-(((x_flat[..., None] - grid) * inv_denom) ** 2))
    bq = mxq(basis.reshape(-1, IN_F * GRID_SIZE), 1, "e4m3")
    wq = mxq(f64(spline_w).reshape(OUT_F, IN_F * GRID_SIZE), 1, "e4m3")
    spline_out = bq @ wq.T
    out = base_out + spline_out
    return out.reshape(*lead, OUT_F)

@@ -1,0 +1,245 @@
+from contextlib import ExitStack
+
+import concourse.mybir as mybir
+from concourse.masks import make_identity
+
+F32 = mybir.dt.float32
+BF16 = mybir.dt.bfloat16
+I32 = mybir.dt.int32
+U32 = mybir.dt.uint32
+U8 = mybir.dt.uint8
+FP8X4 = mybir.dt.float8_e4m3fn_x4
+ACT = mybir.ActivationFunctionType
+ALU = mybir.AluOpType
+
+P = 128
+ROWS = 512
+IN_F = 1024
+OUT_F = 1024
+GRID = 8
+K_PASS = 4 * P
+BASE_PASSES = IN_F // K_PASS
+SPLINE_PASSES = IN_F * GRID // K_PASS
+N_COLS = 512
+COL_HALVES = OUT_F // N_COLS
+ROUNDS = 2
+ROUND_ROWS = ROWS // ROUNDS
+ROUND_TILES = ROUND_ROWS // P
+FEATURE_TILES = IN_F // P
+
+GRID_STEP = 4.0 / 7.0
+INV_DENOM = 1.0 / (GRID_STEP + 1e-06)
+
+FLOPS = 2 * ROWS * OUT_F * (IN_F + IN_F * GRID)
+
+
+def tile_kanlinear_kernel(tc, x, base_w_words, base_w_scales, base_b, spline_w, out):
+    nc = tc.nc
+    x_rows = x.rearrange("b s i -> (b s) i")
+    out_rows = out.rearrange("b s o -> (b s) o")
+    w_rows = spline_w.rearrange("o i g -> o (i g)")
+
+    with ExitStack() as ctx:
+        keep = ctx.enter_context(tc.tile_pool(name="keep", bufs=1))
+        stream = ctx.enter_context(tc.tile_pool(name="stream", bufs=2))
+        psum = ctx.enter_context(tc.psum_pool(name="psum", bufs=2))
+        sums = ctx.enter_context(tc.psum_pool(name="sums", bufs=1))
+
+        x_sb = keep.tile([P, ROWS // P, IN_F], BF16)
+        for rt in range(ROWS // P):
+            nc.sync.dma_start(out=x_sb[:, rt, :], in_=x_rows[rt * P : (rt + 1) * P, :])
+
+        bw_codes = keep.tile([P, BASE_PASSES, OUT_F], U32, align_bytes=64)
+        for c in range(BASE_PASSES):
+            nc.sync.dma_start(
+                out=bw_codes[:, c, :].bitcast(I32),
+                in_=base_w_words[c].rearrange("p n t -> p (n t)").bitcast(I32),
+            )
+        bw_scales = keep.tile([P, BASE_PASSES, OUT_F], U8, align_bytes=64)
+        nc.vector.memset(bw_scales[:].bitcast(I32), 0)
+        for quad in range(4):
+            nc.sync.dma_start(
+                out=bw_scales[32 * quad : 32 * quad + 4, :, :].bitcast(I32),
+                in_=base_w_scales[:, 4 * quad : 4 * quad + 4, :].bitcast(I32).rearrange("c q n -> q c n"),
+            )
+        bias_all = keep.tile([P, OUT_F], BF16)
+        nc.scalar.dma_start(out=bias_all[:], in_=base_b.partition_broadcast(P))
+
+        ident_bf = keep.tile([P, P], BF16)
+        make_identity(nc, ident_bf[:])
+        ident_f32 = keep.tile([P, P], F32)
+        make_identity(nc, ident_f32[:])
+
+        spread = keep.tile([P, P, 4], BF16)
+        nc.vector.tensor_copy(out=spread[:], in_=ident_bf[:].unsqueeze(2).to_broadcast([P, P, 4]))
+        spread_cols = spread[:].rearrange("i j m -> i (j m)")
+
+        point_row = keep.tile([P, P // 4, 4], F32)
+        for m in range(4):
+            nc.vector.memset(point_row[:, :, m], float(2 * m))
+        point_ps = psum.tile([P, P], F32, tag="wt")
+        nc.tensor.transpose(point_ps[:], point_row[:].rearrange("q j m -> q (j m)"), ident_f32[:])
+        shift = keep.tile([P, 2], F32)
+        for e in range(2):
+            nc.vector.tensor_scalar(
+                out=shift[:, e : e + 1],
+                in0=point_ps[:, 0:1],
+                scalar1=-INV_DENOM * GRID_STEP,
+                scalar2=INV_DENOM * (2.0 - GRID_STEP * e),
+                op0=ALU.mult,
+                op1=ALU.add,
+            )
+
+        x_words = x_sb[:].bitcast(F32)
+        act_grouped = keep.tile([P, BASE_PASSES, ROWS, 4], BF16, align_bytes=64)
+        act_codes = keep.tile([P, BASE_PASSES, ROWS], U32, align_bytes=64)
+        act_scales = keep.tile([P, BASE_PASSES, ROWS], U8, align_bytes=64)
+        for rt in range(ROWS // P):
+            xw_ps = psum.tile([P, BASE_PASSES, 2, P], F32, tag="wt")
+            for c in range(BASE_PASSES):
+                for u in range(2):
+                    nc.tensor.transpose(
+                        xw_ps[:, c, u, :], x_words[:, rt, 256 * c + u : 256 * (c + 1) : 2], ident_f32[:]
+                    )
+            for c in range(BASE_PASSES):
+                nc.scalar.activation(
+                    out=act_grouped[:, c, rt * P : (rt + 1) * P, :].rearrange("p r (u e) -> p r u e", u=2),
+                    in_=xw_ps[:, c, :, :].bitcast(BF16).rearrange("p u (r e) -> p r u e", e=2),
+                    func=ACT.Silu,
+                )
+        for rnd in range(ROUNDS):
+            rows = slice(rnd * ROUND_ROWS, (rnd + 1) * ROUND_ROWS)
+            for c in range(BASE_PASSES):
+                nc.vector.quantize_mx(
+                    out=act_codes[:, c, rows].bitcast(FP8X4),
+                    scales=act_scales[:, c, rows],
+                    in_=act_grouped[:, c, rows, :].rearrange("p r t -> p (r t)"),
+                )
+
+        x_t = keep.tile([P, ROUNDS, FEATURE_TILES, ROUND_ROWS], BF16)
+        for rnd in range(ROUNDS):
+            for quarter in range(FEATURE_TILES // 4):
+                xt_ps = psum.tile([P, 4, ROUND_ROWS], BF16, tag="xr")
+                for a in range(4):
+                    ft = 4 * quarter + a
+                    for b in range(ROUND_TILES):
+                        nc.tensor.transpose(
+                            xt_ps[:, a, b * P : (b + 1) * P],
+                            x_sb[:, rnd * ROUND_TILES + b, ft * P : (ft + 1) * P],
+                            ident_bf[:],
+                        )
+                nc.vector.tensor_copy(out=x_t[:, rnd, 4 * quarter : 4 * quarter + 4, :], in_=xt_ps[:])
+
+        basis_codes = keep.tile([P, ROUNDS, SPLINE_PASSES, ROUND_ROWS], U32, align_bytes=64)
+        basis_scales = keep.tile([P, ROUNDS, SPLINE_PASSES, ROUND_ROWS], U8, align_bytes=64)
+        w_codes = keep.tile([P, SPLINE_PASSES, OUT_F], U32, align_bytes=64)
+        w_scales = keep.tile([P, SPLINE_PASSES, OUT_F], U8, align_bytes=64)
+
+        def quantise_basis(rnd, ft):
+            x_spread = psum.tile([P, 4, ROUND_ROWS], BF16, tag="xr")
+            for v in range(4):
+                nc.tensor.matmul(
+                    x_spread[:, v, :],
+                    lhsT=spread_cols[:, v * P : (v + 1) * P],
+                    rhs=x_t[:, rnd, ft, :],
+                    start=True,
+                    stop=True,
+                )
+            squares = stream.tile([P, 2, 4 * ROUND_ROWS], F32)
+            for e in range(2):
+                nc.scalar.activation(
+                    out=squares[:, e, :].rearrange("p (l r u) -> p l r u", l=2, u=2),
+                    in_=x_spread[:].rearrange("p (l u) r -> p l r u", u=2),
+                    func=ACT.Square,
+                    bias=shift[:, e : e + 1],
+                    scale=INV_DENOM,
+                )
+            basis = stream.tile([P, 4 * ROUND_ROWS, 2], BF16, align_bytes=64)
+            nc.scalar.activation(
+                out=basis[:], in_=squares[:].rearrange("p e n -> p n e"), func=ACT.Exp, scale=-1.0
+            )
+            passes = slice(2 * ft, 2 * ft + 2)
+            nc.vector.quantize_mx(
+                out=basis_codes[:, rnd, passes, :].rearrange("p l r -> p (l r)").bitcast(FP8X4),
+                scales=basis_scales[:, rnd, passes, :].rearrange("p l r -> p (l r)"),
+                in_=basis[:].rearrange("p n e -> p (n e)"),
+            )
+
+        def quantise_weights(ft, half):
+            raw = stream.tile([P, 4, 2 * K_PASS], BF16, bufs=3)
+            nc.sync.dma_start(
+                out=raw[:],
+                in_=w_rows[
+                    half * N_COLS : (half + 1) * N_COLS, 2 * ft * K_PASS : 2 * (ft + 1) * K_PASS
+                ].rearrange("(t p) k -> p t k", p=P),
+            )
+            raw_words = raw[:].bitcast(F32)
+            cols = slice(half * N_COLS, (half + 1) * N_COLS)
+            for l in range(2):
+                grouped = stream.tile([P, N_COLS, 4], BF16, bufs=3, align_bytes=64)
+                grouped_words = grouped[:].bitcast(F32)
+                for b in range(2):
+                    wt_ps = psum.tile([P, 2, 2, P], F32, tag="wt")
+                    for a in range(2):
+                        for u in range(2):
+                            first = 256 * l + P * u
+                            nc.tensor.transpose(
+                                wt_ps[:, a, u, :], raw_words[:, 2 * b + a, first : first + P], ident_f32[:]
+                            )
+                    nc.vector.tensor_copy(
+                        out=grouped_words[:, 256 * b : 256 * (b + 1), :].rearrange("p (a o) u -> p a o u", a=2),
+                        in_=wt_ps[:].rearrange("p a u o -> p a o u"),
+                    )
+                nc.vector.quantize_mx(
+                    out=w_codes[:, 2 * ft + l, cols].bitcast(FP8X4),
+                    scales=w_scales[:, 2 * ft + l, cols],
+                    in_=grouped[:].rearrange("p o t -> p (o t)"),
+                )
+
+        for rnd in range(ROUNDS):
+            acc = {}
+            for b in range(ROUND_TILES):
+                for half in range(COL_HALVES):
+                    acc[(b, half)] = sums.tile([P, N_COLS], F32, name="acc%d%d" % (b, half))
+            for c in range(BASE_PASSES):
+                for b in range(ROUND_TILES):
+                    rows = slice((rnd * ROUND_TILES + b) * P, (rnd * ROUND_TILES + b + 1) * P)
+                    for half in range(COL_HALVES):
+                        cols = slice(half * N_COLS, (half + 1) * N_COLS)
+                        nc.tensor.matmul_mx(
+                            out=acc[(b, half)][:],
+                            lhsT=act_codes[:, c, rows].bitcast(FP8X4),
+                            lhsT_scale=act_scales[:, c, rows],
+                            rhs=bw_codes[:, c, cols].bitcast(FP8X4),
+                            rhs_scale=bw_scales[:, c, cols],
+                            start=(c == 0),
+                            stop=False,
+                        )
+            for ft in range(FEATURE_TILES):
+                quantise_basis(rnd, ft)
+                if rnd == 0:
+                    for half in range(COL_HALVES):
+                        quantise_weights(ft, half)
+                for c in range(2 * ft, 2 * ft + 2):
+                    for b in range(ROUND_TILES):
+                        rows = slice(b * P, (b + 1) * P)
+                        for half in range(COL_HALVES):
+                            cols = slice(half * N_COLS, (half + 1) * N_COLS)
+                            nc.tensor.matmul_mx(
+                                out=acc[(b, half)][:],
+                                lhsT=basis_codes[:, rnd, c, rows].bitcast(FP8X4),
+                                lhsT_scale=basis_scales[:, rnd, c, rows],
+                                rhs=w_codes[:, c, cols].bitcast(FP8X4),
+                                rhs_scale=w_scales[:, c, cols],
+                                start=False,
+                                stop=(c == SPLINE_PASSES - 1),
+                            )
+            for b in range(ROUND_TILES):
+                rows = slice((rnd * ROUND_TILES + b) * P, (rnd * ROUND_TILES + b + 1) * P)
+                for half in range(COL_HALVES):
+                    cols = slice(half * N_COLS, (half + 1) * N_COLS)
+                    result = stream.tile([P, N_COLS], F32)
+                    nc.vector.tensor_tensor(
+                        out=result[:], in0=acc[(b, half)][:], in1=bias_all[:, cols], op=ALU.add
+                    )
+                    nc.sync.dma_start(out=out_rows[rows, cols], in_=result[:])

@@ -14,6 +14,7 @@ ALU = mybir.AluOpType
 
 P = 128
 ROWS = 512
+ROW_TILES = ROWS // P
 IN_F = 1024
 OUT_F = 1024
 GRID = 8
@@ -21,16 +22,25 @@ K_PASS = 4 * P
 BASE_PASSES = IN_F // K_PASS
 SPLINE_PASSES = IN_F * GRID // K_PASS
 N_COLS = 512
-COL_HALVES = OUT_F // N_COLS
+HALVES = OUT_F // N_COLS
 ROUNDS = 2
 ROUND_ROWS = ROWS // ROUNDS
 ROUND_TILES = ROUND_ROWS // P
 FEATURE_TILES = IN_F // P
 
+UNITS = ROUNDS * FEATURE_TILES
+ITEMS = HALVES * SPLINE_PASSES
+UNIT_LAG = 2
+ITEM_LAG = 2
+
 GRID_STEP = 4.0 / 7.0
 INV_DENOM = 1.0 / (GRID_STEP + 1e-06)
 
 FLOPS = 2 * ROWS * OUT_F * (IN_F + IN_F * GRID)
+
+
+def items_before(step):
+    return min((5 * step + 1) // 2, ITEMS)
 
 
 def tile_kanlinear_kernel(tc, x, base_w_words, base_w_scales, base_b, spline_w, out):
@@ -40,14 +50,27 @@ def tile_kanlinear_kernel(tc, x, base_w_words, base_w_scales, base_b, spline_w, 
     w_rows = spline_w.rearrange("o i g -> o (i g)")
 
     with ExitStack() as ctx:
+        ctx.enter_context(tc.manual_schedule())
         keep = ctx.enter_context(tc.tile_pool(name="keep", bufs=1))
         stream = ctx.enter_context(tc.tile_pool(name="stream", bufs=2))
         psum = ctx.enter_context(tc.psum_pool(name="psum", bufs=2))
         sums = ctx.enter_context(tc.psum_pool(name="sums", bufs=1))
 
-        x_sb = keep.tile([P, ROWS // P, IN_F], BF16)
-        for rt in range(ROWS // P):
+        def load_weights(chunk):
+            half, ft = divmod(chunk, FEATURE_TILES)
+            raw = stream.tile([P, 4, 2 * K_PASS], BF16, tag="raw", bufs=3)
+            nc.sync.dma_start(
+                out=raw[:],
+                in_=w_rows[
+                    half * N_COLS : (half + 1) * N_COLS, 2 * ft * K_PASS : 2 * (ft + 1) * K_PASS
+                ].rearrange("(t p) k -> p t k", p=P),
+            )
+            return raw
+
+        x_sb = stream.tile([P, ROW_TILES, IN_F], BF16, tag="raw", bufs=3)
+        for rt in range(ROW_TILES):
             nc.sync.dma_start(out=x_sb[:, rt, :], in_=x_rows[rt * P : (rt + 1) * P, :])
+        raw_chunks = {0: load_weights(0), 1: load_weights(1)}
 
         bw_codes = keep.tile([P, BASE_PASSES, OUT_F], U32, align_bytes=64)
         for c in range(BASE_PASSES):
@@ -65,14 +88,10 @@ def tile_kanlinear_kernel(tc, x, base_w_words, base_w_scales, base_b, spline_w, 
         bias_all = keep.tile([P, OUT_F], BF16)
         nc.scalar.dma_start(out=bias_all[:], in_=base_b.partition_broadcast(P))
 
-        ident_bf = keep.tile([P, P], BF16)
-        make_identity(nc, ident_bf[:])
         ident_f32 = keep.tile([P, P], F32)
         make_identity(nc, ident_f32[:])
-
-        spread = keep.tile([P, P, 4], BF16)
-        nc.vector.tensor_copy(out=spread[:], in_=ident_bf[:].unsqueeze(2).to_broadcast([P, P, 4]))
-        spread_cols = spread[:].rearrange("i j m -> i (j m)")
+        ident_bf = keep.tile([P, P], BF16)
+        make_identity(nc, ident_bf[:])
 
         point_row = keep.tile([P, P // 4, 4], F32)
         for m in range(4):
@@ -90,34 +109,32 @@ def tile_kanlinear_kernel(tc, x, base_w_words, base_w_scales, base_b, spline_w, 
                 op1=ALU.add,
             )
 
+        spread = keep.tile([P, P, 4], BF16)
+        nc.vector.tensor_copy(out=spread[:], in_=ident_bf[:].unsqueeze(2).to_broadcast([P, P, 4]))
+        spread_cols = spread[:].rearrange("i j m -> i (j m)")
+
         x_words = x_sb[:].bitcast(F32)
-        act_grouped = keep.tile([P, BASE_PASSES, ROWS, 4], BF16, align_bytes=64)
+        act_grouped = [
+            stream.tile([P, ROWS, 4], BF16, name="act_grouped%d" % c, tag="to_quantise", bufs=4, align_bytes=64)
+            for c in range(BASE_PASSES)
+        ]
         act_codes = keep.tile([P, BASE_PASSES, ROWS], U32, align_bytes=64)
         act_scales = keep.tile([P, BASE_PASSES, ROWS], U8, align_bytes=64)
-        for rt in range(ROWS // P):
-            xw_ps = psum.tile([P, BASE_PASSES, 2, P], F32, tag="wt")
-            for c in range(BASE_PASSES):
-                for u in range(2):
-                    nc.tensor.transpose(
-                        xw_ps[:, c, u, :], x_words[:, rt, 256 * c + u : 256 * (c + 1) : 2], ident_f32[:]
-                    )
-            for c in range(BASE_PASSES):
-                nc.scalar.activation(
-                    out=act_grouped[:, c, rt * P : (rt + 1) * P, :].rearrange("p r (u e) -> p r u e", u=2),
-                    in_=xw_ps[:, c, :, :].bitcast(BF16).rearrange("p u (r e) -> p r u e", e=2),
-                    func=ACT.Silu,
-                )
-        for rnd in range(ROUNDS):
-            rows = slice(rnd * ROUND_ROWS, (rnd + 1) * ROUND_ROWS)
-            for c in range(BASE_PASSES):
-                nc.vector.quantize_mx(
-                    out=act_codes[:, c, rows].bitcast(FP8X4),
-                    scales=act_scales[:, c, rows],
-                    in_=act_grouped[:, c, rows, :].rearrange("p r t -> p (r t)"),
-                )
-
         x_t = keep.tile([P, ROUNDS, FEATURE_TILES, ROUND_ROWS], BF16)
         for rnd in range(ROUNDS):
+            for rt in range(rnd * ROUND_TILES, (rnd + 1) * ROUND_TILES):
+                xw_ps = psum.tile([P, BASE_PASSES, 2, P], F32, tag="wt")
+                for c in range(BASE_PASSES):
+                    for u in range(2):
+                        nc.tensor.transpose(
+                            xw_ps[:, c, u, :], x_words[:, rt, 256 * c + u : 256 * (c + 1) : 2], ident_f32[:]
+                        )
+                for c in range(BASE_PASSES):
+                    nc.scalar.activation(
+                        out=act_grouped[c][:, rt * P : (rt + 1) * P, :].rearrange("p r (u e) -> p r u e", u=2),
+                        in_=xw_ps[:, c, :, :].bitcast(BF16).rearrange("p u (r e) -> p r u e", e=2),
+                        func=ACT.Silu,
+                    )
             for quarter in range(FEATURE_TILES // 4):
                 xt_ps = psum.tile([P, 4, ROUND_ROWS], BF16, tag="xr")
                 for a in range(4):
@@ -130,116 +147,180 @@ def tile_kanlinear_kernel(tc, x, base_w_words, base_w_scales, base_b, spline_w, 
                         )
                 nc.vector.tensor_copy(out=x_t[:, rnd, 4 * quarter : 4 * quarter + 4, :], in_=xt_ps[:])
 
+        def quantise_act(rnd):
+            rows = slice(rnd * ROUND_ROWS, (rnd + 1) * ROUND_ROWS)
+            for c in range(BASE_PASSES):
+                nc.vector.quantize_mx(
+                    out=act_codes[:, c, rows].bitcast(FP8X4),
+                    scales=act_scales[:, c, rows],
+                    in_=act_grouped[c][:, rows, :].rearrange("p r t -> p (r t)"),
+                )
+
         basis_codes = keep.tile([P, ROUNDS, SPLINE_PASSES, ROUND_ROWS], U32, align_bytes=64)
         basis_scales = keep.tile([P, ROUNDS, SPLINE_PASSES, ROUND_ROWS], U8, align_bytes=64)
         w_codes = keep.tile([P, SPLINE_PASSES, OUT_F], U32, align_bytes=64)
         w_scales = keep.tile([P, SPLINE_PASSES, OUT_F], U8, align_bytes=64)
 
-        def quantise_basis(rnd, ft):
-            x_spread = psum.tile([P, 4, ROUND_ROWS], BF16, tag="xr")
+        x_spread = {}
+        basis = {}
+
+        def spread_x(unit):
+            rnd, ft = divmod(unit, FEATURE_TILES)
+            x_spread[unit] = psum.tile([P, 4, ROUND_ROWS], BF16, name="x_spread", tag="xr")
             for v in range(4):
                 nc.tensor.matmul(
-                    x_spread[:, v, :],
+                    x_spread[unit][:, v, :],
                     lhsT=spread_cols[:, v * P : (v + 1) * P],
                     rhs=x_t[:, rnd, ft, :],
                     start=True,
                     stop=True,
                 )
+
+        def basis_values(unit):
             squares = stream.tile([P, 2, 4 * ROUND_ROWS], F32)
             for e in range(2):
                 nc.scalar.activation(
                     out=squares[:, e, :].rearrange("p (l r u) -> p l r u", l=2, u=2),
-                    in_=x_spread[:].rearrange("p (l u) r -> p l r u", u=2),
+                    in_=x_spread[unit][:].rearrange("p (l u) r -> p l r u", u=2),
                     func=ACT.Square,
                     bias=shift[:, e : e + 1],
                     scale=INV_DENOM,
                 )
-            basis = stream.tile([P, 4 * ROUND_ROWS, 2], BF16, align_bytes=64)
-            nc.scalar.activation(
-                out=basis[:], in_=squares[:].rearrange("p e n -> p n e"), func=ACT.Exp, scale=-1.0
+            basis[unit] = stream.tile(
+                [P, 4 * ROUND_ROWS, 2], BF16, name="basis", tag="to_quantise", bufs=4, align_bytes=64
             )
+            nc.scalar.activation(
+                out=basis[unit][:], in_=squares[:].rearrange("p e n -> p n e"), func=ACT.Exp, scale=-1.0
+            )
+
+        def quantise_basis(unit):
+            rnd, ft = divmod(unit, FEATURE_TILES)
             passes = slice(2 * ft, 2 * ft + 2)
             nc.vector.quantize_mx(
                 out=basis_codes[:, rnd, passes, :].rearrange("p l r -> p (l r)").bitcast(FP8X4),
                 scales=basis_scales[:, rnd, passes, :].rearrange("p l r -> p (l r)"),
-                in_=basis[:].rearrange("p n e -> p (n e)"),
+                in_=basis[unit][:].rearrange("p n e -> p (n e)"),
             )
 
-        def quantise_weights(ft, half):
-            raw = stream.tile([P, 4, 2 * K_PASS], BF16, bufs=3)
-            nc.sync.dma_start(
-                out=raw[:],
-                in_=w_rows[
-                    half * N_COLS : (half + 1) * N_COLS, 2 * ft * K_PASS : 2 * (ft + 1) * K_PASS
-                ].rearrange("(t p) k -> p t k", p=P),
-            )
-            raw_words = raw[:].bitcast(F32)
-            cols = slice(half * N_COLS, (half + 1) * N_COLS)
-            for l in range(2):
-                grouped = stream.tile([P, N_COLS, 4], BF16, bufs=3, align_bytes=64)
-                grouped_words = grouped[:].bitcast(F32)
-                for b in range(2):
-                    wt_ps = psum.tile([P, 2, 2, P], F32, tag="wt")
-                    for a in range(2):
-                        for u in range(2):
-                            first = 256 * l + P * u
-                            nc.tensor.transpose(
-                                wt_ps[:, a, u, :], raw_words[:, 2 * b + a, first : first + P], ident_f32[:]
-                            )
-                    nc.vector.tensor_copy(
-                        out=grouped_words[:, 256 * b : 256 * (b + 1), :].rearrange("p (a o) u -> p a o u", a=2),
-                        in_=wt_ps[:].rearrange("p a u o -> p a o u"),
-                    )
-                nc.vector.quantize_mx(
-                    out=w_codes[:, 2 * ft + l, cols].bitcast(FP8X4),
-                    scales=w_scales[:, 2 * ft + l, cols],
-                    in_=grouped[:].rearrange("p o t -> p (o t)"),
+        grouped = {}
+
+        def transpose_weights(item):
+            c = item % SPLINE_PASSES
+            raw_words = raw_chunks[item // 2][:].bitcast(F32)
+            grouped[item] = stream.tile([P, N_COLS, 4], BF16, name="grouped", tag="grouped", bufs=3, align_bytes=64)
+            grouped_words = grouped[item][:].bitcast(F32)
+            banks = []
+            for b in range(2):
+                wt_ps = psum.tile([P, 2, 2, P], F32, tag="wt")
+                banks.append(wt_ps)
+                for a in range(2):
+                    for u in range(2):
+                        first = 256 * (c % 2) + P * u
+                        nc.tensor.transpose(
+                            wt_ps[:, a, u, :], raw_words[:, 2 * b + a, first : first + P], ident_f32[:]
+                        )
+            for b in range(2):
+                nc.vector.tensor_copy(
+                    out=grouped_words[:, 256 * b : 256 * (b + 1), :].rearrange("p (a o) u -> p a o u", a=2),
+                    in_=banks[b][:].rearrange("p a u o -> p a o u"),
                 )
 
-        for rnd in range(ROUNDS):
-            acc = {}
+        def quantise_weights(item):
+            half, c = divmod(item, SPLINE_PASSES)
+            cols = slice(half * N_COLS, (half + 1) * N_COLS)
+            nc.vector.quantize_mx(
+                out=w_codes[:, c, cols].bitcast(FP8X4),
+                scales=w_scales[:, c, cols],
+                in_=grouped[item][:].rearrange("p o t -> p (o t)"),
+            )
+
+        acc = {}
+
+        def open_sums(rnd, half):
+            cols = slice(half * N_COLS, (half + 1) * N_COLS)
             for b in range(ROUND_TILES):
-                for half in range(COL_HALVES):
-                    acc[(b, half)] = sums.tile([P, N_COLS], F32, name="acc%d%d" % (b, half))
+                acc[(half, b)] = sums.tile([P, N_COLS], F32, name="sum%d%d" % (half, b))
             for c in range(BASE_PASSES):
                 for b in range(ROUND_TILES):
                     rows = slice((rnd * ROUND_TILES + b) * P, (rnd * ROUND_TILES + b + 1) * P)
-                    for half in range(COL_HALVES):
-                        cols = slice(half * N_COLS, (half + 1) * N_COLS)
-                        nc.tensor.matmul_mx(
-                            out=acc[(b, half)][:],
-                            lhsT=act_codes[:, c, rows].bitcast(FP8X4),
-                            lhsT_scale=act_scales[:, c, rows],
-                            rhs=bw_codes[:, c, cols].bitcast(FP8X4),
-                            rhs_scale=bw_scales[:, c, cols],
-                            start=(c == 0),
-                            stop=False,
-                        )
-            for ft in range(FEATURE_TILES):
-                quantise_basis(rnd, ft)
-                if rnd == 0:
-                    for half in range(COL_HALVES):
-                        quantise_weights(ft, half)
-                for c in range(2 * ft, 2 * ft + 2):
-                    for b in range(ROUND_TILES):
-                        rows = slice(b * P, (b + 1) * P)
-                        for half in range(COL_HALVES):
-                            cols = slice(half * N_COLS, (half + 1) * N_COLS)
-                            nc.tensor.matmul_mx(
-                                out=acc[(b, half)][:],
-                                lhsT=basis_codes[:, rnd, c, rows].bitcast(FP8X4),
-                                lhsT_scale=basis_scales[:, rnd, c, rows],
-                                rhs=w_codes[:, c, cols].bitcast(FP8X4),
-                                rhs_scale=w_scales[:, c, cols],
-                                start=False,
-                                stop=(c == SPLINE_PASSES - 1),
-                            )
+                    nc.tensor.matmul_mx(
+                        out=acc[(half, b)][:],
+                        lhsT=act_codes[:, c, rows].bitcast(FP8X4),
+                        lhsT_scale=act_scales[:, c, rows],
+                        rhs=bw_codes[:, c, cols].bitcast(FP8X4),
+                        rhs_scale=bw_scales[:, c, cols],
+                        start=(c == 0),
+                        stop=False,
+                    )
+
+        def spline_passes(rnd, half, c):
+            cols = slice(half * N_COLS, (half + 1) * N_COLS)
+            for b in range(ROUND_TILES):
+                rows = slice(b * P, (b + 1) * P)
+                nc.tensor.matmul_mx(
+                    out=acc[(half, b)][:],
+                    lhsT=basis_codes[:, rnd, c, rows].bitcast(FP8X4),
+                    lhsT_scale=basis_scales[:, rnd, c, rows],
+                    rhs=w_codes[:, c, cols].bitcast(FP8X4),
+                    rhs_scale=w_scales[:, c, cols],
+                    start=False,
+                    stop=(c == SPLINE_PASSES - 1),
+                )
+
+        def close_sums(rnd, half):
+            cols = slice(half * N_COLS, (half + 1) * N_COLS)
             for b in range(ROUND_TILES):
                 rows = slice((rnd * ROUND_TILES + b) * P, (rnd * ROUND_TILES + b + 1) * P)
-                for half in range(COL_HALVES):
-                    cols = slice(half * N_COLS, (half + 1) * N_COLS)
-                    result = stream.tile([P, N_COLS], F32)
-                    nc.vector.tensor_tensor(
-                        out=result[:], in0=acc[(b, half)][:], in1=bias_all[:, cols], op=ALU.add
-                    )
-                    nc.sync.dma_start(out=out_rows[rows, cols], in_=result[:])
+                result = stream.tile([P, N_COLS], F32)
+                nc.vector.tensor_tensor(out=result[:], in0=acc[(half, b)][:], in1=bias_all[:, cols], op=ALU.add)
+                nc.sync.dma_start(out=out_rows[rows, cols], in_=result[:])
+
+        def passes_of_item(item):
+            c = item - SPLINE_PASSES
+            if c == 0:
+                open_sums(0, 1)
+            if c >= 0:
+                spline_passes(0, 1, c)
+
+        late_passes = 0
+        spread_x(0)
+        for step in range(UNITS + UNIT_LAG):
+            if step + 1 < UNITS:
+                spread_x(step + 1)
+            if step < UNITS:
+                basis_values(step)
+            if step < ROUNDS:
+                quantise_act(step)
+            unit = step - UNIT_LAG
+            if unit >= 0:
+                quantise_basis(unit)
+            rnd, ft = divmod(max(unit, 0), FEATURE_TILES)
+            items = range(items_before(step), items_before(step + 1))
+            for slot in range(max(2, len(items))):
+                if slot < len(items):
+                    item = items[slot]
+                    if item % 2 == 0 and item // 2 + 2 < ITEMS // 2:
+                        raw_chunks[item // 2 + 2] = load_weights(item // 2 + 2)
+                    transpose_weights(item)
+                    if item >= 1:
+                        quantise_weights(item - 1)
+                    passes_of_item(item - ITEM_LAG)
+                    if item == ITEMS - 1:
+                        quantise_weights(item)
+                        passes_of_item(item - 1)
+                        passes_of_item(item)
+                        close_sums(0, 1)
+                if slot < 2 and unit >= 0:
+                    c = 2 * ft + slot
+                    if c == 0:
+                        open_sums(rnd, 0)
+                    spline_passes(rnd, 0, c)
+                    if c == SPLINE_PASSES - 1:
+                        close_sums(rnd, 0)
+            if unit >= 0 and rnd == 1 and items_before(step) == ITEMS:
+                if late_passes == 0:
+                    open_sums(1, 1)
+                for c in range(late_passes, 2 * ft + 2):
+                    spline_passes(1, 1, c)
+                late_passes = 2 * ft + 2
+        close_sums(1, 1)

@@ -39,10 +39,6 @@ INV_DENOM = 1.0 / (GRID_STEP + 1e-06)
 FLOPS = 2 * ROWS * OUT_F * (IN_F + IN_F * GRID)
 
 
-def items_before(step):
-    return min((5 * step + 1) // 2, ITEMS)
-
-
 def tile_kanlinear_kernel(tc, x, base_w_words, base_w_scales, base_b, spline_w, out):
     nc = tc.nc
     x_rows = x.rearrange("b s i -> (b s) i")
@@ -72,19 +68,6 @@ def tile_kanlinear_kernel(tc, x, base_w_words, base_w_scales, base_b, spline_w, 
             nc.sync.dma_start(out=x_sb[:, rt, :], in_=x_rows[rt * P : (rt + 1) * P, :])
         raw_chunks = {0: load_weights(0), 1: load_weights(1)}
 
-        bw_codes = keep.tile([P, BASE_PASSES, OUT_F], U32, align_bytes=64)
-        for c in range(BASE_PASSES):
-            nc.sync.dma_start(
-                out=bw_codes[:, c, :].bitcast(I32),
-                in_=base_w_words[c].rearrange("p n t -> p (n t)").bitcast(I32),
-            )
-        bw_scales = keep.tile([P, BASE_PASSES, OUT_F], U8, align_bytes=64)
-        nc.vector.memset(bw_scales[:].bitcast(I32), 0)
-        for quad in range(4):
-            nc.sync.dma_start(
-                out=bw_scales[32 * quad : 32 * quad + 4, :, :].bitcast(I32),
-                in_=base_w_scales[:, 4 * quad : 4 * quad + 4, :].bitcast(I32).rearrange("c q n -> q c n"),
-            )
         bias_all = keep.tile([P, OUT_F], BF16)
         nc.scalar.dma_start(out=bias_all[:], in_=base_b.partition_broadcast(P))
 
@@ -109,21 +92,51 @@ def tile_kanlinear_kernel(tc, x, base_w_words, base_w_scales, base_b, spline_w, 
                 op1=ALU.add,
             )
 
-        spread = keep.tile([P, P, 4], BF16)
-        nc.vector.tensor_copy(out=spread[:], in_=ident_bf[:].unsqueeze(2).to_broadcast([P, P, 4]))
-        spread_cols = spread[:].rearrange("i j m -> i (j m)")
+        parked = (
+            out_rows[ROWS - ROUND_ROWS : ROWS, :]
+            .bitcast(BF16)
+            .rearrange("(q a) b -> q (a b)", q=P)
+            .rearrange("q (n f r) -> q n f r", n=ROUNDS, f=FEATURE_TILES)
+        )
+        x_t = keep.tile([P, ROUNDS, FEATURE_TILES, ROUND_ROWS], BF16)
+        x_spread = {}
+
+        def load_x_spread(quad):
+            rnd, first = divmod(4 * quad, FEATURE_TILES)
+            x_spread[quad] = stream.tile([P, 4, 4, ROUND_ROWS], BF16, name="x_spread", tag="x_spread")
+            for v in range(4):
+                nc.sync.dma_start(
+                    out=x_spread[quad][:, v, :, :].rearrange("p a r -> p (a r)"),
+                    in_=parked[32 * v : 32 * (v + 1), rnd, first : first + 4, :]
+                    .rearrange("j a r -> j (a r)")
+                    .unsqueeze(1)
+                    .to_broadcast([32, 4, 4 * ROUND_ROWS]),
+                )
 
         x_words = x_sb[:].bitcast(F32)
         act_grouped = [
             stream.tile([P, ROWS, 4], BF16, name="act_grouped%d" % c, tag="to_quantise", bufs=4, align_bytes=64)
             for c in range(BASE_PASSES)
         ]
-        act_codes = keep.tile([P, BASE_PASSES, ROWS], U32, align_bytes=64)
-        act_scales = keep.tile([P, BASE_PASSES, ROWS], U8, align_bytes=64)
-        x_t = keep.tile([P, ROUNDS, FEATURE_TILES, ROUND_ROWS], BF16)
         for rnd in range(ROUNDS):
-            for rt in range(rnd * ROUND_TILES, (rnd + 1) * ROUND_TILES):
-                xw_ps = psum.tile([P, BASE_PASSES, 2, P], F32, tag="wt")
+            for quarter in range(FEATURE_TILES // 4):
+                xt_ps = sums.tile([P, 4, ROUND_ROWS], BF16, tag="sums_a%d" % quarter)
+                for a in range(4):
+                    ft = 4 * quarter + a
+                    for b in range(ROUND_TILES):
+                        nc.tensor.transpose(
+                            xt_ps[:, a, b * P : (b + 1) * P],
+                            x_sb[:, rnd * ROUND_TILES + b, ft * P : (ft + 1) * P],
+                            ident_bf[:],
+                        )
+                nc.vector.tensor_copy(out=x_t[:, rnd, 4 * quarter : 4 * quarter + 4, :], in_=xt_ps[:])
+            nc.sync.dma_start(out=parked[:, rnd, :, :], in_=x_t[:, rnd, :, :])
+            if rnd == 0:
+                for quad in range(2):
+                    load_x_spread(quad)
+            for b in range(ROUND_TILES):
+                rt = rnd * ROUND_TILES + b
+                xw_ps = sums.tile([P, BASE_PASSES, 2, P], F32, tag="sums_%s%d" % ("bc"[rnd], b))
                 for c in range(BASE_PASSES):
                     for u in range(2):
                         nc.tensor.transpose(
@@ -135,17 +148,23 @@ def tile_kanlinear_kernel(tc, x, base_w_words, base_w_scales, base_b, spline_w, 
                         in_=xw_ps[:, c, :, :].bitcast(BF16).rearrange("p u (r e) -> p r u e", e=2),
                         func=ACT.Silu,
                     )
-            for quarter in range(FEATURE_TILES // 4):
-                xt_ps = psum.tile([P, 4, ROUND_ROWS], BF16, tag="xr")
-                for a in range(4):
-                    ft = 4 * quarter + a
-                    for b in range(ROUND_TILES):
-                        nc.tensor.transpose(
-                            xt_ps[:, a, b * P : (b + 1) * P],
-                            x_sb[:, rnd * ROUND_TILES + b, ft * P : (ft + 1) * P],
-                            ident_bf[:],
-                        )
-                nc.vector.tensor_copy(out=x_t[:, rnd, 4 * quarter : 4 * quarter + 4, :], in_=xt_ps[:])
+
+        bw_codes = keep.tile([P, BASE_PASSES, OUT_F], U32, align_bytes=64)
+        for c in range(BASE_PASSES):
+            nc.sync.dma_start(
+                out=bw_codes[:, c, :].bitcast(I32),
+                in_=base_w_words[c].rearrange("p n t -> p (n t)").bitcast(I32),
+            )
+        bw_scales = keep.tile([P, BASE_PASSES, OUT_F], U8, align_bytes=64)
+        nc.vector.memset(bw_scales[:].bitcast(I32), 0)
+        for quad in range(4):
+            nc.sync.dma_start(
+                out=bw_scales[32 * quad : 32 * quad + 4, :, :].bitcast(I32),
+                in_=base_w_scales[:, 4 * quad : 4 * quad + 4, :].bitcast(I32).rearrange("c q n -> q c n"),
+            )
+
+        act_codes = keep.tile([P, BASE_PASSES, ROWS], U32, align_bytes=64)
+        act_scales = keep.tile([P, BASE_PASSES, ROWS], U8, align_bytes=64)
 
         def quantise_act(rnd):
             rows = slice(rnd * ROUND_ROWS, (rnd + 1) * ROUND_ROWS)
@@ -161,27 +180,14 @@ def tile_kanlinear_kernel(tc, x, base_w_words, base_w_scales, base_b, spline_w, 
         w_codes = keep.tile([P, SPLINE_PASSES, OUT_F], U32, align_bytes=64)
         w_scales = keep.tile([P, SPLINE_PASSES, OUT_F], U8, align_bytes=64)
 
-        x_spread = {}
         basis = {}
-
-        def spread_x(unit):
-            rnd, ft = divmod(unit, FEATURE_TILES)
-            x_spread[unit] = psum.tile([P, 4, ROUND_ROWS], BF16, name="x_spread", tag="xr")
-            for v in range(4):
-                nc.tensor.matmul(
-                    x_spread[unit][:, v, :],
-                    lhsT=spread_cols[:, v * P : (v + 1) * P],
-                    rhs=x_t[:, rnd, ft, :],
-                    start=True,
-                    stop=True,
-                )
 
         def basis_values(unit):
             squares = stream.tile([P, 2, 4 * ROUND_ROWS], F32)
             for e in range(2):
                 nc.scalar.activation(
                     out=squares[:, e, :].rearrange("p (l r u) -> p l r u", l=2, u=2),
-                    in_=x_spread[unit][:].rearrange("p (l u) r -> p l r u", u=2),
+                    in_=x_spread[unit // 4][:, :, unit % 4, :].rearrange("p (l u) r -> p l r u", u=2),
                     func=ACT.Square,
                     bias=shift[:, e : e + 1],
                     scale=INV_DENOM,
@@ -234,17 +240,20 @@ def tile_kanlinear_kernel(tc, x, base_w_words, base_w_scales, base_b, spline_w, 
                 in_=grouped[item][:].rearrange("p o t -> p (o t)"),
             )
 
+        bank_pair = {(0, 0): "a", (0, 1): "b", (1, 0): "c", (1, 1): "a"}
         acc = {}
 
         def open_sums(rnd, half):
             cols = slice(half * N_COLS, (half + 1) * N_COLS)
             for b in range(ROUND_TILES):
-                acc[(half, b)] = sums.tile([P, N_COLS], F32, name="sum%d%d" % (half, b))
+                acc[(rnd, half, b)] = sums.tile(
+                    [P, N_COLS], F32, name="acc", tag="sums_%s%d" % (bank_pair[(rnd, half)], b)
+                )
             for c in range(BASE_PASSES):
                 for b in range(ROUND_TILES):
                     rows = slice((rnd * ROUND_TILES + b) * P, (rnd * ROUND_TILES + b + 1) * P)
                     nc.tensor.matmul_mx(
-                        out=acc[(half, b)][:],
+                        out=acc[(rnd, half, b)][:],
                         lhsT=act_codes[:, c, rows].bitcast(FP8X4),
                         lhsT_scale=act_scales[:, c, rows],
                         rhs=bw_codes[:, c, cols].bitcast(FP8X4),
@@ -258,7 +267,7 @@ def tile_kanlinear_kernel(tc, x, base_w_words, base_w_scales, base_b, spline_w, 
             for b in range(ROUND_TILES):
                 rows = slice(b * P, (b + 1) * P)
                 nc.tensor.matmul_mx(
-                    out=acc[(half, b)][:],
+                    out=acc[(rnd, half, b)][:],
                     lhsT=basis_codes[:, rnd, c, rows].bitcast(FP8X4),
                     lhsT_scale=basis_scales[:, rnd, c, rows],
                     rhs=w_codes[:, c, cols].bitcast(FP8X4),
@@ -272,7 +281,9 @@ def tile_kanlinear_kernel(tc, x, base_w_words, base_w_scales, base_b, spline_w, 
             for b in range(ROUND_TILES):
                 rows = slice((rnd * ROUND_TILES + b) * P, (rnd * ROUND_TILES + b + 1) * P)
                 result = stream.tile([P, N_COLS], F32)
-                nc.vector.tensor_tensor(out=result[:], in0=acc[(half, b)][:], in1=bias_all[:, cols], op=ALU.add)
+                nc.vector.tensor_tensor(
+                    out=result[:], in0=acc[(rnd, half, b)][:], in1=bias_all[:, cols], op=ALU.add
+                )
                 nc.sync.dma_start(out=out_rows[rows, cols], in_=result[:])
 
         def passes_of_item(item):
@@ -282,12 +293,10 @@ def tile_kanlinear_kernel(tc, x, base_w_words, base_w_scales, base_b, spline_w, 
             if c >= 0:
                 spline_passes(0, 1, c)
 
-        late_passes = 0
-        spread_x(0)
         for step in range(UNITS + UNIT_LAG):
-            if step + 1 < UNITS:
-                spread_x(step + 1)
             if step < UNITS:
+                if step % 4 == 0 and 0 < step < UNITS - 4:
+                    load_x_spread(step // 4 + 1)
                 basis_values(step)
             if step < ROUNDS:
                 quantise_act(step)
@@ -295,10 +304,9 @@ def tile_kanlinear_kernel(tc, x, base_w_words, base_w_scales, base_b, spline_w, 
             if unit >= 0:
                 quantise_basis(unit)
             rnd, ft = divmod(max(unit, 0), FEATURE_TILES)
-            items = range(items_before(step), items_before(step + 1))
-            for slot in range(max(2, len(items))):
-                if slot < len(items):
-                    item = items[slot]
+            for slot in range(2):
+                item = 2 * step + slot
+                if item < ITEMS:
                     if item % 2 == 0 and item // 2 + 2 < ITEMS // 2:
                         raw_chunks[item // 2 + 2] = load_weights(item // 2 + 2)
                     transpose_weights(item)
@@ -310,17 +318,11 @@ def tile_kanlinear_kernel(tc, x, base_w_words, base_w_scales, base_b, spline_w, 
                         passes_of_item(item - 1)
                         passes_of_item(item)
                         close_sums(0, 1)
-                if slot < 2 and unit >= 0:
+                if unit >= 0:
                     c = 2 * ft + slot
-                    if c == 0:
-                        open_sums(rnd, 0)
-                    spline_passes(rnd, 0, c)
-                    if c == SPLINE_PASSES - 1:
-                        close_sums(rnd, 0)
-            if unit >= 0 and rnd == 1 and items_before(step) == ITEMS:
-                if late_passes == 0:
-                    open_sums(1, 1)
-                for c in range(late_passes, 2 * ft + 2):
-                    spline_passes(1, 1, c)
-                late_passes = 2 * ft + 2
-        close_sums(1, 1)
+                    for half in range(1 + rnd):
+                        if c == 0:
+                            open_sums(rnd, half)
+                        spline_passes(rnd, half, c)
+                        if c == SPLINE_PASSES - 1:
+                            close_sums(rnd, half)

@@ -14,29 +14,34 @@ ALU = mybir.AluOpType
 
 P = 128
 ROWS = 512
-ROW_TILES = ROWS // P
+ROW_TILES = 4
 IN_F = 1024
 OUT_F = 1024
-GRID = 8
-K_PASS = 4 * P
-BASE_PASSES = IN_F // K_PASS
-SPLINE_PASSES = IN_F * GRID // K_PASS
+K_PASS = 512
+BASE_PASSES = 2
+SPLINE_PASSES = 16
 N_COLS = 512
-HALVES = OUT_F // N_COLS
-ROUNDS = 2
-ROUND_ROWS = ROWS // ROUNDS
-ROUND_TILES = ROUND_ROWS // P
-FEATURE_TILES = IN_F // P
+HALVES = 2
+FEATURE_TILES = 8
+ITEMS = 32
+GROUP_PASSES = BASE_PASSES + SPLINE_PASSES
 
-UNITS = ROUNDS * FEATURE_TILES
-ITEMS = HALVES * SPLINE_PASSES
-UNIT_LAG = 2
-ITEM_LAG = 2
+SKEW = 0
+LAGW = 2
+LAGB = 2
+NP = 4
+LASTMX = 8
+LAST_IN_WT = 1
+BASE_TICK = 6
+RAW_BUFS = 3
 
 GRID_STEP = 4.0 / 7.0
 INV_DENOM = 1.0 / (GRID_STEP + 1e-06)
 
-FLOPS = 2 * ROWS * OUT_F * (IN_F + IN_F * GRID)
+FLOPS = 2 * ROWS * OUT_F * (IN_F + IN_F * 8)
+
+KIND = {"r0": (0, 256), "t2": (256, 128), "t3": (384, 128)}
+WEIGHT = {"r0": 2, "t2": 1, "t3": 1}
 
 
 def tile_kanlinear_kernel(tc, x, base_w_words, base_w_scales, base_b, spline_w, out):
@@ -52,9 +57,15 @@ def tile_kanlinear_kernel(tc, x, base_w_words, base_w_scales, base_b, spline_w, 
         psum = ctx.enter_context(tc.psum_pool(name="psum", bufs=2))
         sums = ctx.enter_context(tc.psum_pool(name="sums", bufs=1))
 
+        chunk_order = [(ft, 0) for ft in range(SKEW)]
+        for ft in range(FEATURE_TILES):
+            if ft + SKEW < FEATURE_TILES:
+                chunk_order.append((ft + SKEW, 0))
+            chunk_order.append((ft, 1))
+
         def load_weights(chunk):
-            half, ft = divmod(chunk, FEATURE_TILES)
-            raw = stream.tile([P, 4, 2 * K_PASS], BF16, tag="raw", bufs=3)
+            ft, half = chunk_order[chunk]
+            raw = stream.tile([P, 4, 2 * K_PASS], BF16, tag="raw", bufs=RAW_BUFS)
             nc.sync.dma_start(
                 out=raw[:],
                 in_=w_rows[
@@ -63,18 +74,21 @@ def tile_kanlinear_kernel(tc, x, base_w_words, base_w_scales, base_b, spline_w, 
             )
             return raw
 
-        x_sb = stream.tile([P, ROW_TILES, IN_F], BF16, tag="raw", bufs=3)
+        x_sb = stream.tile([P, ROW_TILES, IN_F], BF16, tag="raw", bufs=RAW_BUFS)
         for rt in range(ROW_TILES):
             nc.sync.dma_start(out=x_sb[:, rt, :], in_=x_rows[rt * P : (rt + 1) * P, :])
-        raw_chunks = {0: load_weights(0), 1: load_weights(1)}
+        raw_chunks = {0: load_weights(0)}
 
         bias_all = keep.tile([P, OUT_F], BF16)
         nc.scalar.dma_start(out=bias_all[:], in_=base_b.partition_broadcast(P))
 
-        ident_f32 = keep.tile([P, P], F32)
-        make_identity(nc, ident_f32[:])
+        warm = keep.tile([P, 2], F32)
+        nc.vector.memset(warm[:, 0:1], 0.0)
+        nc.scalar.activation(out=warm[:, 1:2], in_=warm[:, 0:1], func=ACT.Silu)
         ident_bf = keep.tile([P, P], BF16)
         make_identity(nc, ident_bf[:])
+        ident_f32 = keep.tile([P, P], F32)
+        make_identity(nc, ident_f32[:])
 
         point_row = keep.tile([P, P // 4, 4], F32)
         for m in range(4):
@@ -92,51 +106,60 @@ def tile_kanlinear_kernel(tc, x, base_w_words, base_w_scales, base_b, spline_w, 
                 op1=ALU.add,
             )
 
-        parked = (
-            out_rows[ROWS - ROUND_ROWS : ROWS, :]
-            .bitcast(BF16)
-            .rearrange("(q a) b -> q (a b)", q=P)
-            .rearrange("q (n f r) -> q n f r", n=ROUNDS, f=FEATURE_TILES)
-        )
-        x_t = keep.tile([P, ROUNDS, FEATURE_TILES, ROUND_ROWS], BF16)
+        parked = out_rows[ROWS - 256 : ROWS, :].bitcast(BF16).rearrange("(q a) b -> q (a b)", q=P)
+        PARK_AT = {"r0": 0, "t2": 2048, "t3": 3072}
+        x_t = [
+            stream.tile([P, 2048], BF16, name="x_t%d" % n, tag="to_quantise", bufs=4, align_bytes=64)
+            for n in range(2)
+        ]
         x_spread = {}
 
-        def load_x_spread(quad):
-            rnd, first = divmod(4 * quad, FEATURE_TILES)
-            x_spread[quad] = stream.tile([P, 4, 4, ROUND_ROWS], BF16, name="x_spread", tag="x_spread")
-            for v in range(4):
-                nc.sync.dma_start(
-                    out=x_spread[quad][:, v, :, :].rearrange("p a r -> p (a r)"),
-                    in_=parked[32 * v : 32 * (v + 1), rnd, first : first + 4, :]
-                    .rearrange("j a r -> j (a r)")
-                    .unsqueeze(1)
-                    .to_broadcast([32, 4, 4 * ROUND_ROWS]),
-                )
+        def load_x_spread(kind, quad, parts=1):
+            rows = KIND[kind][1]
+            t = stream.tile([P, 4, 4, rows], BF16, name="x_spread", tag="xs_" + ("a" if kind == "r0" else "b"))
+            x_spread[(kind, quad)] = t
+            src = parked[:, PARK_AT[kind] + 4 * quad * rows : PARK_AT[kind] + 4 * (quad + 1) * rows]
+            step = 4 // parts
+            for a0 in range(0, 4, step):
+                for v in range(4):
+                    nc.sync.dma_start(
+                        out=t[:, v, a0 : a0 + step, :].rearrange("p a r -> p (a r)"),
+                        in_=src[32 * v : 32 * (v + 1), a0 * rows : (a0 + step) * rows]
+                        .unsqueeze(1)
+                        .to_broadcast([32, 4, step * rows]),
+                    )
 
         x_words = x_sb[:].bitcast(F32)
         act_grouped = [
             stream.tile([P, ROWS, 4], BF16, name="act_grouped%d" % c, tag="to_quantise", bufs=4, align_bytes=64)
             for c in range(BASE_PASSES)
         ]
-        for rnd in range(ROUNDS):
-            for quarter in range(FEATURE_TILES // 4):
-                xt_ps = sums.tile([P, 4, ROUND_ROWS], BF16, tag="sums_a%d" % quarter)
-                for a in range(4):
-                    ft = 4 * quarter + a
-                    for b in range(ROUND_TILES):
+
+        def transpose_x(rnd):
+            for quarter in range(2):
+                xt_ps = sums.tile([P, 2, 4, P], BF16, name="xt_ps", tag="s%d0" % quarter)
+                for b in range(2):
+                    for a in range(4):
+                        ft = 4 * quarter + a
                         nc.tensor.transpose(
-                            xt_ps[:, a, b * P : (b + 1) * P],
-                            x_sb[:, rnd * ROUND_TILES + b, ft * P : (ft + 1) * P],
-                            ident_bf[:],
+                            xt_ps[:, b, a, :], x_sb[:, 2 * rnd + b, ft * P : (ft + 1) * P], ident_bf[:]
                         )
-                nc.vector.tensor_copy(out=x_t[:, rnd, 4 * quarter : 4 * quarter + 4, :], in_=xt_ps[:])
-            nc.sync.dma_start(out=parked[:, rnd, :, :], in_=x_t[:, rnd, :, :])
-            if rnd == 0:
-                for quad in range(2):
-                    load_x_spread(quad)
-            for b in range(ROUND_TILES):
-                rt = rnd * ROUND_TILES + b
-                xw_ps = sums.tile([P, BASE_PASSES, 2, P], F32, tag="sums_%s%d" % ("bc"[rnd], b))
+                if rnd == 0:
+                    nc.vector.tensor_copy(
+                        out=x_t[0][:, 1024 * quarter : 1024 * (quarter + 1)].rearrange("p (a b r) -> p a b r", a=4, b=2),
+                        in_=xt_ps[:].rearrange("p b a r -> p a b r"),
+                    )
+                else:
+                    nc.vector.tensor_copy(
+                        out=x_t[1][:].rearrange("p (b f r) -> p b f r", b=2, f=8)[:, :, 4 * quarter : 4 * quarter + 4, :],
+                        in_=xt_ps[:],
+                    )
+            nc.sync.dma_start(out=parked[:, 2048 * rnd : 2048 * (rnd + 1)], in_=x_t[rnd][:])
+
+        def silu_x(rnd):
+            for b in range(2):
+                rt = 2 * rnd + b
+                xw_ps = sums.tile([P, BASE_PASSES, 2, P], F32, name="xw_ps", tag="s%d1" % (b + rnd) if rnd == 0 else "s%d%d" % (2, b))
                 for c in range(BASE_PASSES):
                     for u in range(2):
                         nc.tensor.transpose(
@@ -149,75 +172,95 @@ def tile_kanlinear_kernel(tc, x, base_w_words, base_w_scales, base_b, spline_w, 
                         func=ACT.Silu,
                     )
 
+        transpose_x(0)
+        raw_chunks[1] = load_weights(1)
+        load_x_spread("r0", 0, parts=4)
+        silu_x(0)
+        transpose_x(1)
+        silu_x(1)
+
         bw_codes = keep.tile([P, BASE_PASSES, OUT_F], U32, align_bytes=64)
-        for c in range(BASE_PASSES):
-            nc.sync.dma_start(
-                out=bw_codes[:, c, :].bitcast(I32),
-                in_=base_w_words[c].rearrange("p n t -> p (n t)").bitcast(I32),
-            )
         bw_scales = keep.tile([P, BASE_PASSES, OUT_F], U8, align_bytes=64)
         nc.vector.memset(bw_scales[:].bitcast(I32), 0)
-        for quad in range(4):
-            nc.sync.dma_start(
-                out=bw_scales[32 * quad : 32 * quad + 4, :, :].bitcast(I32),
-                in_=base_w_scales[:, 4 * quad : 4 * quad + 4, :].bitcast(I32).rearrange("c q n -> q c n"),
-            )
+
+        def load_base_weights():
+            for c in range(BASE_PASSES):
+                nc.sync.dma_start(
+                    out=bw_codes[:, c, :].bitcast(I32),
+                    in_=base_w_words[c].rearrange("p n t -> p (n t)").bitcast(I32),
+                )
+            for quad in range(4):
+                nc.sync.dma_start(
+                    out=bw_scales[32 * quad : 32 * quad + 4, :, :].bitcast(I32),
+                    in_=base_w_scales[:, 4 * quad : 4 * quad + 4, :].bitcast(I32).rearrange("c q n -> q c n"),
+                )
 
         act_codes = keep.tile([P, BASE_PASSES, ROWS], U32, align_bytes=64)
         act_scales = keep.tile([P, BASE_PASSES, ROWS], U8, align_bytes=64)
 
-        def quantise_act(rnd):
-            rows = slice(rnd * ROUND_ROWS, (rnd + 1) * ROUND_ROWS)
-            for c in range(BASE_PASSES):
-                nc.vector.quantize_mx(
-                    out=act_codes[:, c, rows].bitcast(FP8X4),
-                    scales=act_scales[:, c, rows],
-                    in_=act_grouped[c][:, rows, :].rearrange("p r t -> p (r t)"),
-                )
+        def quantise_act(c):
+            nc.vector.quantize_mx(
+                out=act_codes[:, c, :].bitcast(FP8X4),
+                scales=act_scales[:, c, :],
+                in_=act_grouped[c][:].rearrange("p r t -> p (r t)"),
+            )
 
-        basis_codes = keep.tile([P, ROUNDS, SPLINE_PASSES, ROUND_ROWS], U32, align_bytes=64)
-        basis_scales = keep.tile([P, ROUNDS, SPLINE_PASSES, ROUND_ROWS], U8, align_bytes=64)
+        basis_codes = {k: keep.tile([P, SPLINE_PASSES * KIND[k][1]], U32, name="bc_" + k, align_bytes=64) for k in KIND}
+        basis_scales = {k: keep.tile([P, SPLINE_PASSES * KIND[k][1]], U8, name="bs_" + k, align_bytes=64) for k in KIND}
         w_codes = keep.tile([P, SPLINE_PASSES, OUT_F], U32, align_bytes=64)
         w_scales = keep.tile([P, SPLINE_PASSES, OUT_F], U8, align_bytes=64)
 
         basis = {}
+        N_FT = {"r0": 1, "t2": 2, "t3": 2}
 
-        def basis_values(unit):
-            squares = stream.tile([P, 2, 4 * ROUND_ROWS], F32)
+        def basis_values(kind, i):
+            n_ft = N_FT[kind]
+            ft = i * n_ft
+            squares = stream.tile([P, 2, 1024], F32, name="squares", tag="squares")
             for e in range(2):
                 nc.scalar.activation(
-                    out=squares[:, e, :].rearrange("p (l r u) -> p l r u", l=2, u=2),
-                    in_=x_spread[unit // 4][:, :, unit % 4, :].rearrange("p (l u) r -> p l r u", u=2),
+                    out=squares[:, e, :].rearrange("p (l n u) -> p l n u", l=2, u=2),
+                    in_=x_spread[(kind, ft // 4)][:, :, ft % 4 : ft % 4 + n_ft, :].rearrange("p (l u) a r -> p l (a r) u", u=2),
                     func=ACT.Square,
                     bias=shift[:, e : e + 1],
                     scale=INV_DENOM,
                 )
-            basis[unit] = stream.tile(
-                [P, 4 * ROUND_ROWS, 2], BF16, name="basis", tag="to_quantise", bufs=4, align_bytes=64
+            basis[(kind, i)] = stream.tile(
+                [P, 1024, 2], BF16, name="basis", tag="to_quantise", bufs=4, align_bytes=64
             )
             nc.scalar.activation(
-                out=basis[unit][:], in_=squares[:].rearrange("p e n -> p n e"), func=ACT.Exp, scale=-1.0
+                out=basis[(kind, i)][:], in_=squares[:].rearrange("p e n -> p n e"), func=ACT.Exp, scale=-1.0
             )
 
-        def quantise_basis(unit):
-            rnd, ft = divmod(unit, FEATURE_TILES)
-            passes = slice(2 * ft, 2 * ft + 2)
+        def quantise_basis(kind, i):
             nc.vector.quantize_mx(
-                out=basis_codes[:, rnd, passes, :].rearrange("p l r -> p (l r)").bitcast(FP8X4),
-                scales=basis_scales[:, rnd, passes, :].rearrange("p l r -> p (l r)"),
-                in_=basis[unit][:].rearrange("p n e -> p (n e)"),
+                out=basis_codes[kind][:, 512 * i : 512 * (i + 1)].bitcast(FP8X4),
+                scales=basis_scales[kind][:, 512 * i : 512 * (i + 1)],
+                in_=basis[(kind, i)][:].rearrange("p n e -> p (n e)"),
             )
+
+        def basis_slice(rt, c):
+            ft, l = divmod(c, 2)
+            if rt < 2:
+                return "r0", slice(512 * ft + 256 * l + P * rt, 512 * ft + 256 * l + P * (rt + 1))
+            first = 512 * (ft // 2) + 256 * l + P * (ft % 2)
+            return ("t2" if rt == 2 else "t3"), slice(first, first + P)
 
         grouped = {}
 
+        def item_parts(item):
+            chunk, l = divmod(item, 2)
+            ft, half = chunk_order[chunk]
+            return chunk, half, 2 * ft + l
+
         def transpose_weights(item):
-            c = item % SPLINE_PASSES
-            raw_words = raw_chunks[item // 2][:].bitcast(F32)
+            chunk, half, c = item_parts(item)
+            raw_words = raw_chunks[chunk][:].bitcast(F32)
             grouped[item] = stream.tile([P, N_COLS, 4], BF16, name="grouped", tag="grouped", bufs=3, align_bytes=64)
             grouped_words = grouped[item][:].bitcast(F32)
             banks = []
             for b in range(2):
-                wt_ps = psum.tile([P, 2, 2, P], F32, tag="wt")
+                wt_ps = psum.tile([P, 2, 2, P], F32, name="wt_ps", tag="wt")
                 banks.append(wt_ps)
                 for a in range(2):
                     for u in range(2):
@@ -232,7 +275,7 @@ def tile_kanlinear_kernel(tc, x, base_w_words, base_w_scales, base_b, spline_w, 
                 )
 
         def quantise_weights(item):
-            half, c = divmod(item, SPLINE_PASSES)
+            chunk, half, c = item_parts(item)
             cols = slice(half * N_COLS, (half + 1) * N_COLS)
             nc.vector.quantize_mx(
                 out=w_codes[:, c, cols].bitcast(FP8X4),
@@ -240,89 +283,134 @@ def tile_kanlinear_kernel(tc, x, base_w_words, base_w_scales, base_b, spline_w, 
                 in_=grouped[item][:].rearrange("p o t -> p (o t)"),
             )
 
-        bank_pair = {(0, 0): "a", (0, 1): "b", (1, 0): "c", (1, 1): "a"}
         acc = {}
+        done = {}
 
-        def open_sums(rnd, half):
+        def one_pass(rt, half, lhsT, lhsT_scale, rhs, rhs_scale):
+            key = (rt, half)
+            n = done.get(key, 0)
+            nc.tensor.matmul_mx(
+                out=acc[key][:], lhsT=lhsT, lhsT_scale=lhsT_scale, rhs=rhs, rhs_scale=rhs_scale,
+                start=(n == 0), stop=(n == GROUP_PASSES - 1),
+            )
+            done[key] = n + 1
+
+        def base_passes(tiles, half):
             cols = slice(half * N_COLS, (half + 1) * N_COLS)
-            for b in range(ROUND_TILES):
-                acc[(rnd, half, b)] = sums.tile(
-                    [P, N_COLS], F32, name="acc", tag="sums_%s%d" % (bank_pair[(rnd, half)], b)
-                )
             for c in range(BASE_PASSES):
-                for b in range(ROUND_TILES):
-                    rows = slice((rnd * ROUND_TILES + b) * P, (rnd * ROUND_TILES + b + 1) * P)
-                    nc.tensor.matmul_mx(
-                        out=acc[(rnd, half, b)][:],
-                        lhsT=act_codes[:, c, rows].bitcast(FP8X4),
-                        lhsT_scale=act_scales[:, c, rows],
-                        rhs=bw_codes[:, c, cols].bitcast(FP8X4),
-                        rhs_scale=bw_scales[:, c, cols],
-                        start=(c == 0),
-                        stop=False,
-                    )
+                for rt in tiles:
+                    rows = slice(rt * P, (rt + 1) * P)
+                    one_pass(rt, half, act_codes[:, c, rows].bitcast(FP8X4), act_scales[:, c, rows],
+                             bw_codes[:, c, cols].bitcast(FP8X4), bw_scales[:, c, cols])
 
-        def spline_passes(rnd, half, c):
+        def spline_passes(tiles, half, c):
             cols = slice(half * N_COLS, (half + 1) * N_COLS)
-            for b in range(ROUND_TILES):
-                rows = slice(b * P, (b + 1) * P)
-                nc.tensor.matmul_mx(
-                    out=acc[(rnd, half, b)][:],
-                    lhsT=basis_codes[:, rnd, c, rows].bitcast(FP8X4),
-                    lhsT_scale=basis_scales[:, rnd, c, rows],
-                    rhs=w_codes[:, c, cols].bitcast(FP8X4),
-                    rhs_scale=w_scales[:, c, cols],
-                    start=False,
-                    stop=(c == SPLINE_PASSES - 1),
-                )
+            for rt in tiles:
+                kind, rows = basis_slice(rt, c)
+                one_pass(rt, half, basis_codes[kind][:, rows].bitcast(FP8X4), basis_scales[kind][:, rows],
+                         w_codes[:, c, cols].bitcast(FP8X4), w_scales[:, c, cols])
 
-        def close_sums(rnd, half):
+        def close_sums(rt, half):
             cols = slice(half * N_COLS, (half + 1) * N_COLS)
-            for b in range(ROUND_TILES):
-                rows = slice((rnd * ROUND_TILES + b) * P, (rnd * ROUND_TILES + b + 1) * P)
-                result = stream.tile([P, N_COLS], F32)
-                nc.vector.tensor_tensor(
-                    out=result[:], in0=acc[(rnd, half, b)][:], in1=bias_all[:, cols], op=ALU.add
-                )
-                nc.sync.dma_start(out=out_rows[rows, cols], in_=result[:])
+            rows = slice(rt * P, (rt + 1) * P)
+            result = stream.tile([P, N_COLS], F32, name="result", tag="result", bufs=3)
+            nc.vector.tensor_tensor(out=result[:], in0=acc[(rt, half)][:], in1=bias_all[:, cols], op=ALU.add)
+            nc.sync.dma_start(out=out_rows[rows, cols], in_=result[:])
 
-        def passes_of_item(item):
-            c = item - SPLINE_PASSES
-            if c == 0:
-                open_sums(0, 1)
-            if c >= 0:
-                spline_passes(0, 1, c)
-
-        for step in range(UNITS + UNIT_LAG):
-            if step < UNITS:
-                if step % 4 == 0 and 0 < step < UNITS - 4:
-                    load_x_spread(step // 4 + 1)
-                basis_values(step)
-            if step < ROUNDS:
-                quantise_act(step)
-            unit = step - UNIT_LAG
-            if unit >= 0:
-                quantise_basis(unit)
-            rnd, ft = divmod(max(unit, 0), FEATURE_TILES)
-            for slot in range(2):
-                item = 2 * step + slot
-                if item < ITEMS:
-                    if item % 2 == 0 and item // 2 + 2 < ITEMS // 2:
-                        raw_chunks[item // 2 + 2] = load_weights(item // 2 + 2)
-                    transpose_weights(item)
-                    if item >= 1:
-                        quantise_weights(item - 1)
-                    passes_of_item(item - ITEM_LAG)
-                    if item == ITEMS - 1:
-                        quantise_weights(item)
-                        passes_of_item(item - 1)
-                        passes_of_item(item)
-                        close_sums(0, 1)
-                if unit >= 0:
-                    c = 2 * ft + slot
-                    for half in range(1 + rnd):
-                        if c == 0:
-                            open_sums(rnd, half)
-                        spline_passes(rnd, half, c)
-                        if c == SPLINE_PASSES - 1:
-                            close_sums(rnd, half)
+        units = []
+        for q in range(4):
+            units += [("r0", 2 * q), ("t2", q), ("r0", 2 * q + 1)]
+        units += [("t3", q) for q in range(4)]
+        start_tick = {}
+        quant_tick = {}
+        for n, u in enumerate(units):
+            start_tick[u] = 2 * n
+            quant_tick[u] = 2 * n + 2 + LAGB
+        lock = (0, 1, 2)
+        quantised = {}
+        item_of = {}
+        for i in range(ITEMS):
+            chunk, half, c = item_parts(i)
+            item_of[(c, half)] = i
+        pending = [("base", 0), ("base", 1)] + [("pass", (i, rt)) for i in range(ITEMS) for rt in lock]
+        last = [("base", 0), ("base", 1)] + [("pass", (c, h)) for c in range(SPLINE_PASSES) for h in range(HALVES)]
+        to_close = []
+        closed = []
+        tick = 0
+        while pending or last or to_close:
+            assert tick < 60
+            if tick == 0:
+                raw_chunks[2] = load_weights(2)
+                load_x_spread("t2", 0)
+            if tick == 3:
+                load_base_weights()
+            if tick == 5:
+                load_x_spread("r0", 1)
+            if tick == 7:
+                load_x_spread("t2", 1)
+            if tick < ITEMS and tick % 2 == 0 and tick >= 2 and tick // 2 + 2 < ITEMS // 2:
+                raw_chunks[tick // 2 + 2] = load_weights(tick // 2 + 2)
+            if tick < ITEMS:
+                transpose_weights(tick)
+            if 1 <= tick <= ITEMS:
+                quantise_weights(tick - 1)
+                quantised[("item", tick - 1)] = tick
+            if tick < BASE_PASSES:
+                quantise_act(tick)
+            for u in units:
+                if quant_tick[u] == tick:
+                    quantise_basis(*u)
+                    quantised[u] = tick
+            for u in units:
+                if start_tick[u] == tick:
+                    if u[0] == "t3" and u[1] % 2 == 0:
+                        load_x_spread("t3", u[1] // 2)
+                    basis_values(*u)
+            for k in to_close[:1]:
+                close_sums(*k)
+                closed.append(k)
+            to_close = to_close[1:]
+            n = 0
+            while pending and n < NP:
+                what, i = pending[0]
+                if what == "base":
+                    if tick < BASE_TICK:
+                        break
+                    for rt in lock:
+                        acc[(rt, i)] = sums.tile([P, N_COLS], F32, name="acc", tag="s%d%d" % (rt, i))
+                    base_passes(lock, i)
+                    n += 6
+                else:
+                    item, rt = i
+                    chunk, half, c = item_parts(item)
+                    unit = ("r0", c // 2) if rt < 2 else ("t2", c // 4)
+                    if item > tick - LAGW or quantised.get(unit, 99) >= tick:
+                        break
+                    spline_passes((rt,), half, c)
+                    if done[(rt, half)] == GROUP_PASSES:
+                        to_close.append((rt, half))
+                    n += 1
+                pending = pending[1:]
+            n = 0
+            while last and n < LASTMX:
+                what, i = last[0]
+                if what == "base":
+                    if LAST_IN_WT:
+                        if tick <= ITEMS:
+                            break
+                        acc[(3, i)] = psum.tile([P, N_COLS], F32, name="acc", tag="wt")
+                    else:
+                        if (i, 0) not in closed:
+                            break
+                        acc[(3, i)] = sums.tile([P, N_COLS], F32, name="acc", tag="s%d0" % i)
+                    base_passes((3,), i)
+                else:
+                    c, half = i
+                    if quantised.get(("t3", c // 4), 99) >= tick or quantised.get(("item", item_of[i]), 99) >= tick:
+                        break
+                    spline_passes((3,), half, c)
+                    if c == SPLINE_PASSES - 1:
+                        to_close += [(3, half)]
+                last = last[1:]
+                n += 1
+            tick += 1

@@ -32,8 +32,16 @@ LAGB = 2
 NP = 4
 LASTMX = 8
 LAST_IN_WT = 1
-BASE_TICK = 6
+BASE_TICK = 7
 RAW_BUFS = 3
+HEAD_A = 0
+HEAD_B = 1
+T3_LATE = 1
+UNIT0 = 2
+BW_TICK = 3
+XS_FIRST = 4
+XS_STEP = 4
+SPREAD_PARTS = 1
 
 GRID_STEP = 4.0 / 7.0
 INV_DENOM = 1.0 / (GRID_STEP + 1e-06)
@@ -74,10 +82,10 @@ def tile_kanlinear_kernel(tc, x, base_w_words, base_w_scales, base_b, spline_w, 
             )
             return raw
 
-        x_sb = stream.tile([P, ROW_TILES, IN_F], BF16, tag="raw", bufs=RAW_BUFS)
-        for rt in range(ROW_TILES):
-            nc.sync.dma_start(out=x_sb[:, rt, :], in_=x_rows[rt * P : (rt + 1) * P, :])
+        x_sb = stream.tile([P, ROW_TILES, IN_F], BF16, tag="squares", bufs=3)
+        nc.sync.dma_start(out=x_sb[:, 0:2, :], in_=x_rows[0 : 2 * P, :].rearrange("(t p) i -> p t i", p=P))
         raw_chunks = {0: load_weights(0)}
+        nc.sync.dma_start(out=x_sb[:, 2:4, :], in_=x_rows[2 * P : 4 * P, :].rearrange("(t p) i -> p t i", p=P))
 
         bias_all = keep.tile([P, OUT_F], BF16)
         nc.scalar.dma_start(out=bias_all[:], in_=base_b.partition_broadcast(P))
@@ -114,13 +122,14 @@ def tile_kanlinear_kernel(tc, x, base_w_words, base_w_scales, base_b, spline_w, 
         ]
         x_spread = {}
 
-        def load_x_spread(kind, quad, parts=1):
+        def load_x_spread(kind, i, parts=1):
             rows = KIND[kind][1]
-            t = stream.tile([P, 4, 4, rows], BF16, name="x_spread", tag="xs_" + ("a" if kind == "r0" else "b"))
-            x_spread[(kind, quad)] = t
-            src = parked[:, PARK_AT[kind] + 4 * quad * rows : PARK_AT[kind] + 4 * (quad + 1) * rows]
-            step = 4 // parts
-            for a0 in range(0, 4, step):
+            n_ft = 512 // rows
+            t = stream.tile([P, 4, n_ft, rows], BF16, name="x_spread", tag="xs", bufs=4)
+            x_spread[(kind, i)] = t
+            src = parked[:, PARK_AT[kind] + 512 * i : PARK_AT[kind] + 512 * (i + 1)]
+            step = n_ft // parts
+            for a0 in range(0, n_ft, step):
                 for v in range(4):
                     nc.sync.dma_start(
                         out=t[:, v, a0 : a0 + step, :].rearrange("p a r -> p (a r)"),
@@ -174,10 +183,8 @@ def tile_kanlinear_kernel(tc, x, base_w_words, base_w_scales, base_b, spline_w, 
 
         transpose_x(0)
         raw_chunks[1] = load_weights(1)
-        load_x_spread("r0", 0, parts=4)
+        load_x_spread("r0", 0, parts=SPREAD_PARTS)
         silu_x(0)
-        transpose_x(1)
-        silu_x(1)
 
         bw_codes = keep.tile([P, BASE_PASSES, OUT_F], U32, align_bytes=64)
         bw_scales = keep.tile([P, BASE_PASSES, OUT_F], U8, align_bytes=64)
@@ -213,23 +220,28 @@ def tile_kanlinear_kernel(tc, x, base_w_words, base_w_scales, base_b, spline_w, 
         basis = {}
         N_FT = {"r0": 1, "t2": 2, "t3": 2}
 
-        def basis_values(kind, i):
+        squares = {}
+
+        def basis_squares(kind, i):
             n_ft = N_FT[kind]
             ft = i * n_ft
-            squares = stream.tile([P, 2, 1024], F32, name="squares", tag="squares")
+            per = 512 // KIND[kind][1]
+            squares[(kind, i)] = stream.tile([P, 2, 1024], F32, name="squares", tag="squares", bufs=3)
             for e in range(2):
                 nc.scalar.activation(
-                    out=squares[:, e, :].rearrange("p (l n u) -> p l n u", l=2, u=2),
-                    in_=x_spread[(kind, ft // 4)][:, :, ft % 4 : ft % 4 + n_ft, :].rearrange("p (l u) a r -> p l (a r) u", u=2),
+                    out=squares[(kind, i)][:, e, :].rearrange("p (l n u) -> p l n u", l=2, u=2),
+                    in_=x_spread[(kind, ft // per)][:, :, ft % per : ft % per + n_ft, :].rearrange("p (l u) a r -> p l (a r) u", u=2),
                     func=ACT.Square,
                     bias=shift[:, e : e + 1],
                     scale=INV_DENOM,
                 )
+
+        def basis_exp(kind, i):
             basis[(kind, i)] = stream.tile(
                 [P, 1024, 2], BF16, name="basis", tag="to_quantise", bufs=4, align_bytes=64
             )
             nc.scalar.activation(
-                out=basis[(kind, i)][:], in_=squares[:].rearrange("p e n -> p n e"), func=ACT.Exp, scale=-1.0
+                out=basis[(kind, i)][:], in_=squares[(kind, i)][:].rearrange("p e n -> p n e"), func=ACT.Exp, scale=-1.0
             )
 
         def quantise_basis(kind, i):
@@ -295,6 +307,12 @@ def tile_kanlinear_kernel(tc, x, base_w_words, base_w_scales, base_b, spline_w, 
             )
             done[key] = n + 1
 
+        def base_pass(rt, half, c):
+            cols = slice(half * N_COLS, (half + 1) * N_COLS)
+            rows = slice(rt * P, (rt + 1) * P)
+            one_pass(rt, half, act_codes[:, c, rows].bitcast(FP8X4), act_scales[:, c, rows],
+                     bw_codes[:, c, cols].bitcast(FP8X4), bw_scales[:, c, cols])
+
         def base_passes(tiles, half):
             cols = slice(half * N_COLS, (half + 1) * N_COLS)
             for c in range(BASE_PASSES):
@@ -319,20 +337,29 @@ def tile_kanlinear_kernel(tc, x, base_w_words, base_w_scales, base_b, spline_w, 
 
         units = []
         for q in range(4):
-            units += [("r0", 2 * q), ("t2", q), ("r0", 2 * q + 1)]
+            units += [("r0", 2 * q), ("r0", 2 * q + 1), ("t2", q)]
         units += [("t3", q) for q in range(4)]
         start_tick = {}
         quant_tick = {}
         for n, u in enumerate(units):
-            start_tick[u] = 2 * n
-            quant_tick[u] = 2 * n + 2 + LAGB
+            start_tick[u] = 2 * n + UNIT0
+            quant_tick[u] = 2 * n + UNIT0 + 2 + LAGB
+            if T3_LATE and u[0] == "t3":
+                quant_tick[u] = max(quant_tick[u], ITEMS + 1 + u[1])
         lock = (0, 1, 2)
+        spreads = [("r0", 1), ("r0", 2), ("t2", 1), ("r0", 3), ("t3", 0), ("t3", 1)]
         quantised = {}
         item_of = {}
         for i in range(ITEMS):
             chunk, half, c = item_parts(i)
             item_of[(c, half)] = i
-        pending = [("base", 0), ("base", 1)] + [("pass", (i, rt)) for i in range(ITEMS) for rt in lock]
+        queues = []
+        for tiles in ((0, 1), (2,)):
+            queues.append(
+                [("base", (c, h), rt) for h in range(HALVES) for c in range(BASE_PASSES) for rt in tiles]
+                + [("pass", i, rt) for i in range(ITEMS) for rt in tiles]
+            )
+        pending = queues[0] + queues[1]
         last = [("base", 0), ("base", 1)] + [("pass", (c, h)) for c in range(SPLINE_PASSES) for h in range(HALVES)]
         to_close = []
         closed = []
@@ -341,56 +368,70 @@ def tile_kanlinear_kernel(tc, x, base_w_words, base_w_scales, base_b, spline_w, 
             assert tick < 60
             if tick == 0:
                 raw_chunks[2] = load_weights(2)
-                load_x_spread("t2", 0)
-            if tick == 3:
-                load_base_weights()
-            if tick == 5:
-                load_x_spread("r0", 1)
-            if tick == 7:
-                load_x_spread("t2", 1)
             if tick < ITEMS and tick % 2 == 0 and tick >= 2 and tick // 2 + 2 < ITEMS // 2:
                 raw_chunks[tick // 2 + 2] = load_weights(tick // 2 + 2)
+            if tick == 2:
+                load_x_spread("t2", 0)
+            if tick == BW_TICK:
+                load_base_weights()
+            for k, s in enumerate(spreads):
+                if tick == XS_FIRST + XS_STEP * k:
+                    load_x_spread(*s)
             if tick < ITEMS:
                 transpose_weights(tick)
             if 1 <= tick <= ITEMS:
                 quantise_weights(tick - 1)
                 quantised[("item", tick - 1)] = tick
-            if tick < BASE_PASSES:
-                quantise_act(tick)
+            if tick == HEAD_A:
+                transpose_x(1)
+            if tick == HEAD_B:
+                silu_x(1)
+            if HEAD_B < tick <= HEAD_B + BASE_PASSES:
+                quantise_act(tick - HEAD_B - 1)
             for u in units:
                 if quant_tick[u] == tick:
                     quantise_basis(*u)
                     quantised[u] = tick
-            for u in units:
+            for n, u in enumerate(units):
                 if start_tick[u] == tick:
-                    if u[0] == "t3" and u[1] % 2 == 0:
-                        load_x_spread("t3", u[1] // 2)
-                    basis_values(*u)
+                    basis_squares(*u)
+                    if n == 0:
+                        basis_exp(*u)
+                    if n >= 2:
+                        basis_exp(*units[n - 1])
+            if tick == start_tick[units[-1]] + 2:
+                basis_exp(*units[-1])
             for k in to_close[:1]:
                 close_sums(*k)
                 closed.append(k)
             to_close = to_close[1:]
             n = 0
-            while pending and n < NP:
-                what, i = pending[0]
-                if what == "base":
-                    if tick < BASE_TICK:
-                        break
-                    for rt in lock:
-                        acc[(rt, i)] = sums.tile([P, N_COLS], F32, name="acc", tag="s%d%d" % (rt, i))
-                    base_passes(lock, i)
-                    n += 6
-                else:
-                    item, rt = i
-                    chunk, half, c = item_parts(item)
-                    unit = ("r0", c // 2) if rt < 2 else ("t2", c // 4)
-                    if item > tick - LAGW or quantised.get(unit, 99) >= tick:
-                        break
-                    spline_passes((rt,), half, c)
+            moved = True
+            while moved and n < NP:
+                moved = False
+                for k in range(2):
+                    if not queues[k] or n >= NP:
+                        continue
+                    what, i, rt = queues[k][0]
+                    if what == "base":
+                        if tick < BASE_TICK:
+                            continue
+                        c, half = i
+                        if (rt, half) not in acc:
+                            acc[(rt, half)] = sums.tile([P, N_COLS], F32, name="acc", tag="s%d%d" % (rt, half))
+                        base_pass(rt, half, c)
+                    else:
+                        chunk, half, c = item_parts(i)
+                        unit = ("r0", c // 2) if rt < 2 else ("t2", c // 4)
+                        if i > tick - LAGW or quantised.get(unit, 99) >= tick:
+                            continue
+                        spline_passes((rt,), half, c)
                     if done[(rt, half)] == GROUP_PASSES:
                         to_close.append((rt, half))
+                    queues[k] = queues[k][1:]
                     n += 1
-                pending = pending[1:]
+                    moved = True
+            pending = queues[0] + queues[1]
             n = 0
             while last and n < LASTMX:
                 what, i = last[0]

@@ -27,8 +27,8 @@ ITEMS = 32
 GROUP_PASSES = BASE_PASSES + SPLINE_PASSES
 
 SKEW = 0
-LAGW = 2
-LAGB = 2
+LAGW = 3
+LAGB = 3
 NP = 4
 LASTMX = 8
 LAST_IN_WT = 1

@@ -168,7 +168,7 @@ def tile_kanlinear_kernel(tc, x, base_w_words, base_w_scales, base_b, spline_w, 
         def silu_x(rnd):
             for b in range(2):
                 rt = 2 * rnd + b
-                xw_ps = sums.tile([P, BASE_PASSES, 2, P], F32, name="xw_ps", tag="s%d1" % (b + rnd) if rnd == 0 else "s%d%d" % (2, b))
+                xw_ps = sums.tile([P, BASE_PASSES, 2, P], F32, name="xw_ps", tag="s%d1" % b)
                 for c in range(BASE_PASSES):
                     for u in range(2):
                         nc.tensor.transpose(
@@ -181,10 +181,25 @@ def tile_kanlinear_kernel(tc, x, base_w_words, base_w_scales, base_b, spline_w, 
                         func=ACT.Silu,
                     )
 
+        sel = keep.tile([P, 4, 32, 4], BF16)
+        for v in range(4):
+            nc.vector.tensor_copy(
+                out=sel[:, v, :, :], in_=ident_bf[:, 32 * v : 32 * (v + 1)].unsqueeze(2).to_broadcast([P, 32, 4])
+            )
         transpose_x(0)
         raw_chunks[1] = load_weights(1)
-        load_x_spread("r0", 0, parts=SPREAD_PARTS)
         silu_x(0)
+        first_x = {}
+
+        def spread_first():
+            for ft in range(2):
+                first_x[ft] = sums.tile([P, 4, 256], BF16, name="first_x", tag="s2%d" % ft)
+                for v in range(4):
+                    nc.tensor.matmul(
+                        out=first_x[ft][:, v, :], lhsT=sel[:, v, :, :].rearrange("p i m -> p (i m)"),
+                        rhs=x_t[0][:, 256 * ft : 256 * (ft + 1)], start=True, stop=True,
+                    )
+
 
         bw_codes = keep.tile([P, BASE_PASSES, OUT_F], U32, align_bytes=64)
         bw_scales = keep.tile([P, BASE_PASSES, OUT_F], U8, align_bytes=64)
@@ -230,7 +245,11 @@ def tile_kanlinear_kernel(tc, x, base_w_words, base_w_scales, base_b, spline_w, 
             for e in range(2):
                 nc.scalar.activation(
                     out=squares[(kind, i)][:, e, :].rearrange("p (l n u) -> p l n u", l=2, u=2),
-                    in_=x_spread[(kind, ft // per)][:, :, ft % per : ft % per + n_ft, :].rearrange("p (l u) a r -> p l (a r) u", u=2),
+                    in_=(
+                        first_x[ft][:].rearrange("p (l u) r -> p l r u", u=2)
+                        if kind == "r0" and ft < 2
+                        else x_spread[(kind, ft // per)][:, :, ft % per : ft % per + n_ft, :].rearrange("p (l u) a r -> p l (a r) u", u=2)
+                    ),
                     func=ACT.Square,
                     bias=shift[:, e : e + 1],
                     scale=INV_DENOM,
@@ -386,6 +405,7 @@ def tile_kanlinear_kernel(tc, x, base_w_words, base_w_scales, base_b, spline_w, 
                 transpose_x(1)
             if tick == HEAD_B:
                 silu_x(1)
+                spread_first()
             if HEAD_B < tick <= HEAD_B + BASE_PASSES:
                 quantise_act(tick - HEAD_B - 1)
             for u in units:

@@ -87,8 +87,13 @@ def tile_kanlinear_kernel(tc, x, base_w_words, base_w_scales, base_b, spline_w, 
         raw_chunks = {0: load_weights(0)}
         nc.sync.dma_start(out=x_sb[:, 2:4, :], in_=x_rows[2 * P : 4 * P, :].rearrange("(t p) i -> p t i", p=P))
 
-        bias_all = keep.tile([P, OUT_F], BF16)
-        nc.scalar.dma_start(out=bias_all[:], in_=base_b.partition_broadcast(P))
+        bias_tiles = []
+
+        def load_bias():
+            bias_all = stream.tile([P, OUT_F], BF16, tag="raw", bufs=RAW_BUFS)
+            nc.sync.dma_start(out=bias_all[:], in_=base_b.partition_broadcast(P))
+            bias_tiles.append(bias_all)
+
 
         warm = keep.tile([P, 2], F32)
         nc.vector.memset(warm[:, 0:1], 0.0)
@@ -351,7 +356,7 @@ def tile_kanlinear_kernel(tc, x, base_w_words, base_w_scales, base_b, spline_w, 
             cols = slice(half * N_COLS, (half + 1) * N_COLS)
             rows = slice(rt * P, (rt + 1) * P)
             result = stream.tile([P, N_COLS], F32, name="result", tag="result", bufs=3)
-            nc.vector.tensor_tensor(out=result[:], in0=acc[(rt, half)][:], in1=bias_all[:, cols], op=ALU.add)
+            nc.vector.tensor_tensor(out=result[:], in0=acc[(rt, half)][:], in1=bias_tiles[0][:, cols], op=ALU.add)
             nc.sync.dma_start(out=out_rows[rows, cols], in_=result[:])
 
         units = []
@@ -393,6 +398,8 @@ def tile_kanlinear_kernel(tc, x, base_w_words, base_w_scales, base_b, spline_w, 
                 load_x_spread("t2", 0)
             if tick == BW_TICK:
                 load_base_weights()
+            if tick == ITEMS - 4:
+                load_bias()
             for k, s in enumerate(spreads):
                 if tick == XS_FIRST + XS_STEP * k:
                     load_x_spread(*s)

@@ -38,6 +38,7 @@ HEAD_A = 0
 HEAD_B = 1
 T3_LATE = 1
 UNIT0 = 2
+WARM = 5
 BW_TICK = 3
 XS_FIRST = 4
 XS_STEP = 4
@@ -102,6 +103,11 @@ def tile_kanlinear_kernel(tc, x, base_w_words, base_w_scales, base_b, spline_w, 
         make_identity(nc, ident_bf[:])
         ident_f32 = keep.tile([P, P], F32)
         make_identity(nc, ident_f32[:])
+        zeros = stream.tile([P, N_COLS], BF16, tag="result", bufs=3)
+        nc.vector.memset(zeros[:], 0.0)
+        warm_ps = psum.tile([P, N_COLS], F32, tag="wt")
+        for k in range(WARM):
+            nc.tensor.matmul(out=warm_ps[:], lhsT=ident_bf[:], rhs=zeros[:], start=True, stop=True)
 
         point_row = keep.tile([P, P // 4, 4], F32)
         for m in range(4):

@@ -38,9 +38,10 @@ HEAD_A = 0
 HEAD_B = 1
 T3_LATE = 1
 UNIT0 = 2
+SPLIT_LAST = 1
 WARM = 5
 BW_TICK = 3
-XS_FIRST = 4
+XS_FIRST = 5
 XS_STEP = 4
 SPREAD_PARTS = 1
 
@@ -109,7 +110,7 @@ def tile_kanlinear_kernel(tc, x, base_w_words, base_w_scales, base_b, spline_w, 
         for k in range(WARM):
             nc.tensor.matmul(out=warm_ps[:], lhsT=ident_bf[:], rhs=zeros[:], start=True, stop=True)
 
-        point_row = keep.tile([P, P // 4, 4], F32)
+        point_row = stream.tile([P, P // 4, 4], F32, tag="result", bufs=3)
         for m in range(4):
             nc.vector.memset(point_row[:, :, m], float(2 * m))
         point_ps = psum.tile([P, P], F32, tag="wt")
@@ -125,20 +126,17 @@ def tile_kanlinear_kernel(tc, x, base_w_words, base_w_scales, base_b, spline_w, 
                 op1=ALU.add,
             )
 
-        parked = out_rows[ROWS - 256 : ROWS, :].bitcast(BF16).rearrange("(q a) b -> q (a b)", q=P)
         PARK_AT = {"r0": 0, "t2": 2048, "t3": 3072}
-        x_t = [
-            stream.tile([P, 2048], BF16, name="x_t%d" % n, tag="to_quantise", bufs=4, align_bytes=64)
-            for n in range(2)
-        ]
+        x_t = [keep.tile([P, 2048], BF16, name="x_t%d" % n) for n in range(2)]
         x_spread = {}
 
         def load_x_spread(kind, i, parts=1):
             rows = KIND[kind][1]
             n_ft = 512 // rows
-            t = stream.tile([P, 4, n_ft, rows], BF16, name="x_spread", tag="xs", bufs=4)
+            t = stream.tile([P, 4, n_ft, rows], BF16, name="x_spread", tag="xs", bufs=3)
             x_spread[(kind, i)] = t
-            src = parked[:, PARK_AT[kind] + 512 * i : PARK_AT[kind] + 512 * (i + 1)]
+            at = PARK_AT[kind] + 512 * i
+            src = x_t[at // 2048][:, at % 2048 : at % 2048 + 512]
             step = n_ft // parts
             for a0 in range(0, n_ft, step):
                 for v in range(4):
@@ -174,7 +172,6 @@ def tile_kanlinear_kernel(tc, x, base_w_words, base_w_scales, base_b, spline_w, 
                         out=x_t[1][:].rearrange("p (b f r) -> p b f r", b=2, f=8)[:, :, 4 * quarter : 4 * quarter + 4, :],
                         in_=xt_ps[:],
                     )
-            nc.sync.dma_start(out=parked[:, 2048 * rnd : 2048 * (rnd + 1)], in_=x_t[rnd][:])
 
         def silu_x(rnd):
             for b in range(2):
@@ -192,7 +189,7 @@ def tile_kanlinear_kernel(tc, x, base_w_words, base_w_scales, base_b, spline_w, 
                         func=ACT.Silu,
                     )
 
-        sel = keep.tile([P, 4, 32, 4], BF16)
+        sel = stream.tile([P, 4, 32, 4], BF16, tag="grouped", bufs=3, align_bytes=64)
         for v in range(4):
             nc.vector.tensor_copy(
                 out=sel[:, v, :, :], in_=ident_bf[:, 32 * v : 32 * (v + 1)].unsqueeze(2).to_broadcast([P, 32, 4])
@@ -270,15 +267,20 @@ def tile_kanlinear_kernel(tc, x, base_w_words, base_w_scales, base_b, spline_w, 
             basis[(kind, i)] = stream.tile(
                 [P, 1024, 2], BF16, name="basis", tag="to_quantise", bufs=4, align_bytes=64
             )
-            nc.scalar.activation(
-                out=basis[(kind, i)][:], in_=squares[(kind, i)][:].rearrange("p e n -> p n e"), func=ACT.Exp, scale=-1.0
-            )
+            parts = 2 if (SPLIT_LAST and (kind, i) == units[-1]) else 1
+            for l in range(parts):
+                cols = slice(1024 // parts * l, 1024 // parts * (l + 1))
+                nc.scalar.activation(
+                    out=basis[(kind, i)][:, cols, :], in_=squares[(kind, i)][:, :, cols].rearrange("p e n -> p n e"),
+                    func=ACT.Exp, scale=-1.0,
+                )
 
-        def quantise_basis(kind, i):
+        def quantise_basis(kind, i, first=0, parts=1):
+            n = 512 // parts
             nc.vector.quantize_mx(
-                out=basis_codes[kind][:, 512 * i : 512 * (i + 1)].bitcast(FP8X4),
-                scales=basis_scales[kind][:, 512 * i : 512 * (i + 1)],
-                in_=basis[(kind, i)][:].rearrange("p n e -> p (n e)"),
+                out=basis_codes[kind][:, 512 * i + n * first : 512 * i + n * (first + 1)].bitcast(FP8X4),
+                scales=basis_scales[kind][:, 512 * i + n * first : 512 * i + n * (first + 1)],
+                in_=basis[(kind, i)][:, 2 * n * first : 2 * n * (first + 1), :].rearrange("p n e -> p (n e)"),
             )
 
         def basis_slice(rt, c):
@@ -390,7 +392,11 @@ def tile_kanlinear_kernel(tc, x, base_w_words, base_w_scales, base_b, spline_w, 
                 + [("pass", i, rt) for i in range(ITEMS) for rt in tiles]
             )
         pending = queues[0] + queues[1]
-        last = [("base", 0), ("base", 1)] + [("pass", (c, h)) for c in range(SPLINE_PASSES) for h in range(HALVES)]
+        last = [("base", 0), ("base", 1)] + [("pass", (c, h)) for c in range(SPLINE_PASSES - 4) for h in range(HALVES)]
+        if SPLIT_LAST:
+            last += [("pass", (c, h)) for c in (12, 14) for h in range(HALVES)] + [("pass", (c, h)) for h in range(HALVES) for c in (13, 15)]
+        else:
+            last += [("pass", (c, h)) for c in range(SPLINE_PASSES - 4, SPLINE_PASSES) for h in range(HALVES)]
         to_close = []
         closed = []
         tick = 0
@@ -423,8 +429,15 @@ def tile_kanlinear_kernel(tc, x, base_w_words, base_w_scales, base_b, spline_w, 
                 quantise_act(tick - HEAD_B - 1)
             for u in units:
                 if quant_tick[u] == tick:
-                    quantise_basis(*u)
-                    quantised[u] = tick
+                    if SPLIT_LAST and u == units[-1]:
+                        quantise_basis(u[0], u[1], 0, 2)
+                        quantised[(u, 0)] = tick
+                    else:
+                        quantise_basis(*u)
+                        quantised[u] = tick
+                if SPLIT_LAST and u == units[-1] and quant_tick[u] + 1 == tick:
+                    quantise_basis(u[0], u[1], 1, 2)
+                    quantised[(u, 1)] = tick
             for n, u in enumerate(units):
                 if start_tick[u] == tick:
                     basis_squares(*u)
@@ -480,10 +493,13 @@ def tile_kanlinear_kernel(tc, x, base_w_words, base_w_scales, base_b, spline_w, 
                     base_passes((3,), i)
                 else:
                     c, half = i
-                    if quantised.get(("t3", c // 4), 99) >= tick or quantised.get(("item", item_of[i]), 99) >= tick:
+                    unit = ("t3", c // 4)
+                    if SPLIT_LAST and unit == units[-1]:
+                        unit = (unit, c % 2)
+                    if quantised.get(unit, 99) >= tick or quantised.get(("item", item_of[i]), 99) >= tick:
                         break
                     spline_passes((3,), half, c)
-                    if c == SPLINE_PASSES - 1:
+                    if done[(3, half)] == GROUP_PASSES:
                         to_close += [(3, half)]
                 last = last[1:]
                 n += 1

from contextlib import ExitStack

import concourse.mybir as mybir
from concourse.masks import make_identity

F32 = mybir.dt.float32
BF16 = mybir.dt.bfloat16
I32 = mybir.dt.int32
U32 = mybir.dt.uint32
U8 = mybir.dt.uint8
FP8X4 = mybir.dt.float8_e4m3fn_x4
ACT = mybir.ActivationFunctionType
ALU = mybir.AluOpType

P = 128
ROWS = 512
ROW_TILES = 4
IN_F = 1024
OUT_F = 1024
K_PASS = 512
BASE_PASSES = 2
SPLINE_PASSES = 16
N_COLS = 512
HALVES = 2
FEATURE_TILES = 8
ITEMS = 32
GROUP_PASSES = BASE_PASSES + SPLINE_PASSES

SKEW = 0
LAGW = 3
LAGB = 3
NP = 4
LASTMX = 8
LAST_IN_WT = 1
BASE_TICK = 7
RAW_BUFS = 3
HEAD_A = 0
HEAD_B = 1
T3_LATE = 1
UNIT0 = 2
SPLIT_LAST = 1
WARM = 5
BW_TICK = 3
XS_FIRST = 5
XS_STEP = 4
SPREAD_PARTS = 1

GRID_STEP = 4.0 / 7.0
INV_DENOM = 1.0 / (GRID_STEP + 1e-06)

FLOPS = 2 * ROWS * OUT_F * (IN_F + IN_F * 8)

KIND = {"r0": (0, 256), "t2": (256, 128), "t3": (384, 128)}
WEIGHT = {"r0": 2, "t2": 1, "t3": 1}


def tile_kanlinear_kernel(tc, x, base_w_words, base_w_scales, base_b, spline_w, out):
    nc = tc.nc
    x_rows = x.rearrange("b s i -> (b s) i")
    out_rows = out.rearrange("b s o -> (b s) o")
    w_rows = spline_w.rearrange("o i g -> o (i g)")

    with ExitStack() as ctx:
        ctx.enter_context(tc.manual_schedule())
        keep = ctx.enter_context(tc.tile_pool(name="keep", bufs=1))
        stream = ctx.enter_context(tc.tile_pool(name="stream", bufs=2))
        psum = ctx.enter_context(tc.psum_pool(name="psum", bufs=2))
        sums = ctx.enter_context(tc.psum_pool(name="sums", bufs=1))

        chunk_order = [(ft, 0) for ft in range(SKEW)]
        for ft in range(FEATURE_TILES):
            if ft + SKEW < FEATURE_TILES:
                chunk_order.append((ft + SKEW, 0))
            chunk_order.append((ft, 1))

        def load_weights(chunk):
            ft, half = chunk_order[chunk]
            raw = stream.tile([P, 4, 2 * K_PASS], BF16, tag="raw", bufs=RAW_BUFS)
            nc.sync.dma_start(
                out=raw[:],
                in_=w_rows[
                    half * N_COLS : (half + 1) * N_COLS, 2 * ft * K_PASS : 2 * (ft + 1) * K_PASS
                ].rearrange("(t p) k -> p t k", p=P),
            )
            return raw

        x_sb = stream.tile([P, ROW_TILES, IN_F], BF16, tag="squares", bufs=3)
        nc.sync.dma_start(out=x_sb[:, 0:2, :], in_=x_rows[0 : 2 * P, :].rearrange("(t p) i -> p t i", p=P))
        raw_chunks = {0: load_weights(0)}
        nc.sync.dma_start(out=x_sb[:, 2:4, :], in_=x_rows[2 * P : 4 * P, :].rearrange("(t p) i -> p t i", p=P))

        bias_tiles = []

        def load_bias():
            bias_all = stream.tile([P, OUT_F], BF16, tag="raw", bufs=RAW_BUFS)
            nc.sync.dma_start(out=bias_all[:], in_=base_b.partition_broadcast(P))
            bias_tiles.append(bias_all)


        warm = keep.tile([P, 2], F32)
        nc.vector.memset(warm[:, 0:1], 0.0)
        nc.scalar.activation(out=warm[:, 1:2], in_=warm[:, 0:1], func=ACT.Silu)
        ident_bf = keep.tile([P, P], BF16)
        make_identity(nc, ident_bf[:])
        ident_f32 = keep.tile([P, P], F32)
        make_identity(nc, ident_f32[:])
        zeros = stream.tile([P, N_COLS], BF16, tag="result", bufs=3)
        nc.vector.memset(zeros[:], 0.0)
        warm_ps = psum.tile([P, N_COLS], F32, tag="wt")
        for k in range(WARM):
            nc.tensor.matmul(out=warm_ps[:], lhsT=ident_bf[:], rhs=zeros[:], start=True, stop=True)

        point_row = stream.tile([P, P // 4, 4], F32, tag="result", bufs=3)
        for m in range(4):
            nc.vector.memset(point_row[:, :, m], float(2 * m))
        point_ps = psum.tile([P, P], F32, tag="wt")
        nc.tensor.transpose(point_ps[:], point_row[:].rearrange("q j m -> q (j m)"), ident_f32[:])
        shift = keep.tile([P, 2], F32)
        for e in range(2):
            nc.vector.tensor_scalar(
                out=shift[:, e : e + 1],
                in0=point_ps[:, 0:1],
                scalar1=-INV_DENOM * GRID_STEP,
                scalar2=INV_DENOM * (2.0 - GRID_STEP * e),
                op0=ALU.mult,
                op1=ALU.add,
            )

        PARK_AT = {"r0": 0, "t2": 2048, "t3": 3072}
        x_t = [keep.tile([P, 2048], BF16, name="x_t%d" % n) for n in range(2)]
        x_spread = {}

        def load_x_spread(kind, i, parts=1):
            rows = KIND[kind][1]
            n_ft = 512 // rows
            t = stream.tile([P, 4, n_ft, rows], BF16, name="x_spread", tag="xs", bufs=3)
            x_spread[(kind, i)] = t
            at = PARK_AT[kind] + 512 * i
            src = x_t[at // 2048][:, at % 2048 : at % 2048 + 512]
            step = n_ft // parts
            for a0 in range(0, n_ft, step):
                for v in range(4):
                    nc.sync.dma_start(
                        out=t[:, v, a0 : a0 + step, :].rearrange("p a r -> p (a r)"),
                        in_=src[32 * v : 32 * (v + 1), a0 * rows : (a0 + step) * rows]
                        .unsqueeze(1)
                        .to_broadcast([32, 4, step * rows]),
                    )

        x_words = x_sb[:].bitcast(F32)
        act_grouped = [
            stream.tile([P, ROWS, 4], BF16, name="act_grouped%d" % c, tag="to_quantise", bufs=4, align_bytes=64)
            for c in range(BASE_PASSES)
        ]

        def transpose_x(rnd):
            for quarter in range(2):
                xt_ps = sums.tile([P, 2, 4, P], BF16, name="xt_ps", tag="s%d0" % quarter)
                for b in range(2):
                    for a in range(4):
                        ft = 4 * quarter + a
                        nc.tensor.transpose(
                            xt_ps[:, b, a, :], x_sb[:, 2 * rnd + b, ft * P : (ft + 1) * P], ident_bf[:]
                        )
                if rnd == 0:
                    nc.vector.tensor_copy(
                        out=x_t[0][:, 1024 * quarter : 1024 * (quarter + 1)].rearrange("p (a b r) -> p a b r", a=4, b=2),
                        in_=xt_ps[:].rearrange("p b a r -> p a b r"),
                    )
                else:
                    nc.vector.tensor_copy(
                        out=x_t[1][:].rearrange("p (b f r) -> p b f r", b=2, f=8)[:, :, 4 * quarter : 4 * quarter + 4, :],
                        in_=xt_ps[:],
                    )

        def silu_x(rnd):
            for b in range(2):
                rt = 2 * rnd + b
                xw_ps = sums.tile([P, BASE_PASSES, 2, P], F32, name="xw_ps", tag="s%d1" % b)
                for c in range(BASE_PASSES):
                    for u in range(2):
                        nc.tensor.transpose(
                            xw_ps[:, c, u, :], x_words[:, rt, 256 * c + u : 256 * (c + 1) : 2], ident_f32[:]
                        )
                for c in range(BASE_PASSES):
                    nc.scalar.activation(
                        out=act_grouped[c][:, rt * P : (rt + 1) * P, :].rearrange("p r (u e) -> p r u e", u=2),
                        in_=xw_ps[:, c, :, :].bitcast(BF16).rearrange("p u (r e) -> p r u e", e=2),
                        func=ACT.Silu,
                    )

        sel = stream.tile([P, 4, 32, 4], BF16, tag="grouped", bufs=3, align_bytes=64)
        for v in range(4):
            nc.vector.tensor_copy(
                out=sel[:, v, :, :], in_=ident_bf[:, 32 * v : 32 * (v + 1)].unsqueeze(2).to_broadcast([P, 32, 4])
            )
        transpose_x(0)
        raw_chunks[1] = load_weights(1)
        silu_x(0)
        first_x = {}

        def spread_first():
            for ft in range(2):
                first_x[ft] = sums.tile([P, 4, 256], BF16, name="first_x", tag="s2%d" % ft)
                for v in range(4):
                    nc.tensor.matmul(
                        out=first_x[ft][:, v, :], lhsT=sel[:, v, :, :].rearrange("p i m -> p (i m)"),
                        rhs=x_t[0][:, 256 * ft : 256 * (ft + 1)], start=True, stop=True,
                    )


        bw_codes = keep.tile([P, BASE_PASSES, OUT_F], U32, align_bytes=64)
        bw_scales = keep.tile([P, BASE_PASSES, OUT_F], U8, align_bytes=64)
        nc.vector.memset(bw_scales[:].bitcast(I32), 0)

        def load_base_weights():
            for c in range(BASE_PASSES):
                nc.sync.dma_start(
                    out=bw_codes[:, c, :].bitcast(I32),
                    in_=base_w_words[c].rearrange("p n t -> p (n t)").bitcast(I32),
                )
            for quad in range(4):
                nc.sync.dma_start(
                    out=bw_scales[32 * quad : 32 * quad + 4, :, :].bitcast(I32),
                    in_=base_w_scales[:, 4 * quad : 4 * quad + 4, :].bitcast(I32).rearrange("c q n -> q c n"),
                )

        act_codes = keep.tile([P, BASE_PASSES, ROWS], U32, align_bytes=64)
        act_scales = keep.tile([P, BASE_PASSES, ROWS], U8, align_bytes=64)

        def quantise_act(c):
            nc.vector.quantize_mx(
                out=act_codes[:, c, :].bitcast(FP8X4),
                scales=act_scales[:, c, :],
                in_=act_grouped[c][:].rearrange("p r t -> p (r t)"),
            )

        basis_codes = {k: keep.tile([P, SPLINE_PASSES * KIND[k][1]], U32, name="bc_" + k, align_bytes=64) for k in KIND}
        basis_scales = {k: keep.tile([P, SPLINE_PASSES * KIND[k][1]], U8, name="bs_" + k, align_bytes=64) for k in KIND}
        w_codes = keep.tile([P, SPLINE_PASSES, OUT_F], U32, align_bytes=64)
        w_scales = keep.tile([P, SPLINE_PASSES, OUT_F], U8, align_bytes=64)

        basis = {}
        N_FT = {"r0": 1, "t2": 2, "t3": 2}

        squares = {}

        def basis_squares(kind, i):
            n_ft = N_FT[kind]
            ft = i * n_ft
            per = 512 // KIND[kind][1]
            squares[(kind, i)] = stream.tile([P, 2, 1024], F32, name="squares", tag="squares", bufs=3)
            for e in range(2):
                nc.scalar.activation(
                    out=squares[(kind, i)][:, e, :].rearrange("p (l n u) -> p l n u", l=2, u=2),
                    in_=(
                        first_x[ft][:].rearrange("p (l u) r -> p l r u", u=2)
                        if kind == "r0" and ft < 2
                        else x_spread[(kind, ft // per)][:, :, ft % per : ft % per + n_ft, :].rearrange("p (l u) a r -> p l (a r) u", u=2)
                    ),
                    func=ACT.Square,
                    bias=shift[:, e : e + 1],
                    scale=INV_DENOM,
                )

        def basis_exp(kind, i):
            basis[(kind, i)] = stream.tile(
                [P, 1024, 2], BF16, name="basis", tag="to_quantise", bufs=4, align_bytes=64
            )
            parts = 2 if (SPLIT_LAST and (kind, i) == units[-1]) else 1
            for l in range(parts):
                cols = slice(1024 // parts * l, 1024 // parts * (l + 1))
                nc.scalar.activation(
                    out=basis[(kind, i)][:, cols, :], in_=squares[(kind, i)][:, :, cols].rearrange("p e n -> p n e"),
                    func=ACT.Exp, scale=-1.0,
                )

        def quantise_basis(kind, i, first=0, parts=1):
            n = 512 // parts
            nc.vector.quantize_mx(
                out=basis_codes[kind][:, 512 * i + n * first : 512 * i + n * (first + 1)].bitcast(FP8X4),
                scales=basis_scales[kind][:, 512 * i + n * first : 512 * i + n * (first + 1)],
                in_=basis[(kind, i)][:, 2 * n * first : 2 * n * (first + 1), :].rearrange("p n e -> p (n e)"),
            )

        def basis_slice(rt, c):
            ft, l = divmod(c, 2)
            if rt < 2:
                return "r0", slice(512 * ft + 256 * l + P * rt, 512 * ft + 256 * l + P * (rt + 1))
            first = 512 * (ft // 2) + 256 * l + P * (ft % 2)
            return ("t2" if rt == 2 else "t3"), slice(first, first + P)

        grouped = {}

        def item_parts(item):
            chunk, l = divmod(item, 2)
            ft, half = chunk_order[chunk]
            return chunk, half, 2 * ft + l

        def transpose_weights(item):
            chunk, half, c = item_parts(item)
            raw_words = raw_chunks[chunk][:].bitcast(F32)
            grouped[item] = stream.tile([P, N_COLS, 4], BF16, name="grouped", tag="grouped", bufs=3, align_bytes=64)
            grouped_words = grouped[item][:].bitcast(F32)
            banks = []
            for b in range(2):
                wt_ps = psum.tile([P, 2, 2, P], F32, name="wt_ps", tag="wt")
                banks.append(wt_ps)
                for a in range(2):
                    for u in range(2):
                        first = 256 * (c % 2) + P * u
                        nc.tensor.transpose(
                            wt_ps[:, a, u, :], raw_words[:, 2 * b + a, first : first + P], ident_f32[:]
                        )
            for b in range(2):
                nc.vector.tensor_copy(
                    out=grouped_words[:, 256 * b : 256 * (b + 1), :].rearrange("p (a o) u -> p a o u", a=2),
                    in_=banks[b][:].rearrange("p a u o -> p a o u"),
                )

        def quantise_weights(item):
            chunk, half, c = item_parts(item)
            cols = slice(half * N_COLS, (half + 1) * N_COLS)
            nc.vector.quantize_mx(
                out=w_codes[:, c, cols].bitcast(FP8X4),
                scales=w_scales[:, c, cols],
                in_=grouped[item][:].rearrange("p o t -> p (o t)"),
            )

        acc = {}
        done = {}

        def one_pass(rt, half, lhsT, lhsT_scale, rhs, rhs_scale):
            key = (rt, half)
            n = done.get(key, 0)
            nc.tensor.matmul_mx(
                out=acc[key][:], lhsT=lhsT, lhsT_scale=lhsT_scale, rhs=rhs, rhs_scale=rhs_scale,
                start=(n == 0), stop=(n == GROUP_PASSES - 1),
            )
            done[key] = n + 1

        def base_pass(rt, half, c):
            cols = slice(half * N_COLS, (half + 1) * N_COLS)
            rows = slice(rt * P, (rt + 1) * P)
            one_pass(rt, half, act_codes[:, c, rows].bitcast(FP8X4), act_scales[:, c, rows],
                     bw_codes[:, c, cols].bitcast(FP8X4), bw_scales[:, c, cols])

        def base_passes(tiles, half):
            cols = slice(half * N_COLS, (half + 1) * N_COLS)
            for c in range(BASE_PASSES):
                for rt in tiles:
                    rows = slice(rt * P, (rt + 1) * P)
                    one_pass(rt, half, act_codes[:, c, rows].bitcast(FP8X4), act_scales[:, c, rows],
                             bw_codes[:, c, cols].bitcast(FP8X4), bw_scales[:, c, cols])

        def spline_passes(tiles, half, c):
            cols = slice(half * N_COLS, (half + 1) * N_COLS)
            for rt in tiles:
                kind, rows = basis_slice(rt, c)
                one_pass(rt, half, basis_codes[kind][:, rows].bitcast(FP8X4), basis_scales[kind][:, rows],
                         w_codes[:, c, cols].bitcast(FP8X4), w_scales[:, c, cols])

        def close_sums(rt, half):
            cols = slice(half * N_COLS, (half + 1) * N_COLS)
            rows = slice(rt * P, (rt + 1) * P)
            result = stream.tile([P, N_COLS], F32, name="result", tag="result", bufs=3)
            nc.vector.tensor_tensor(out=result[:], in0=acc[(rt, half)][:], in1=bias_tiles[0][:, cols], op=ALU.add)
            nc.sync.dma_start(out=out_rows[rows, cols], in_=result[:])

        units = []
        for q in range(4):
            units += [("r0", 2 * q), ("r0", 2 * q + 1), ("t2", q)]
        units += [("t3", q) for q in range(4)]
        start_tick = {}
        quant_tick = {}
        for n, u in enumerate(units):
            start_tick[u] = 2 * n + UNIT0
            quant_tick[u] = 2 * n + UNIT0 + 2 + LAGB
            if T3_LATE and u[0] == "t3":
                quant_tick[u] = max(quant_tick[u], ITEMS + 1 + u[1])
        lock = (0, 1, 2)
        spreads = [("r0", 1), ("r0", 2), ("t2", 1), ("r0", 3), ("t3", 0), ("t3", 1)]
        quantised = {}
        item_of = {}
        for i in range(ITEMS):
            chunk, half, c = item_parts(i)
            item_of[(c, half)] = i
        queues = []
        for tiles in ((0, 1), (2,)):
            queues.append(
                [("base", (c, h), rt) for h in range(HALVES) for c in range(BASE_PASSES) for rt in tiles]
                + [("pass", i, rt) for i in range(ITEMS) for rt in tiles]
            )
        pending = queues[0] + queues[1]
        last = [("base", 0), ("base", 1)] + [("pass", (c, h)) for c in range(SPLINE_PASSES - 4) for h in range(HALVES)]
        if SPLIT_LAST:
            last += [("pass", (c, h)) for c in (12, 14) for h in range(HALVES)] + [("pass", (c, h)) for h in range(HALVES) for c in (13, 15)]
        else:
            last += [("pass", (c, h)) for c in range(SPLINE_PASSES - 4, SPLINE_PASSES) for h in range(HALVES)]
        to_close = []
        closed = []
        tick = 0
        while pending or last or to_close:
            assert tick < 60
            if tick == 0:
                raw_chunks[2] = load_weights(2)
            if tick < ITEMS and tick % 2 == 0 and tick >= 2 and tick // 2 + 2 < ITEMS // 2:
                raw_chunks[tick // 2 + 2] = load_weights(tick // 2 + 2)
            if tick == 2:
                load_x_spread("t2", 0)
            if tick == BW_TICK:
                load_base_weights()
            if tick == ITEMS - 4:
                load_bias()
            for k, s in enumerate(spreads):
                if tick == XS_FIRST + XS_STEP * k:
                    load_x_spread(*s)
            if tick < ITEMS:
                transpose_weights(tick)
            if 1 <= tick <= ITEMS:
                quantise_weights(tick - 1)
                quantised[("item", tick - 1)] = tick
            if tick == HEAD_A:
                transpose_x(1)
            if tick == HEAD_B:
                silu_x(1)
                spread_first()
            if HEAD_B < tick <= HEAD_B + BASE_PASSES:
                quantise_act(tick - HEAD_B - 1)
            for u in units:
                if quant_tick[u] == tick:
                    if SPLIT_LAST and u == units[-1]:
                        quantise_basis(u[0], u[1], 0, 2)
                        quantised[(u, 0)] = tick
                    else:
                        quantise_basis(*u)
                        quantised[u] = tick
                if SPLIT_LAST and u == units[-1] and quant_tick[u] + 1 == tick:
                    quantise_basis(u[0], u[1], 1, 2)
                    quantised[(u, 1)] = tick
            for n, u in enumerate(units):
                if start_tick[u] == tick:
                    basis_squares(*u)
                    if n == 0:
                        basis_exp(*u)
                    if n >= 2:
                        basis_exp(*units[n - 1])
            if tick == start_tick[units[-1]] + 2:
                basis_exp(*units[-1])
            for k in to_close[:1]:
                close_sums(*k)
                closed.append(k)
            to_close = to_close[1:]
            n = 0
            moved = True
            while moved and n < NP:
                moved = False
                for k in range(2):
                    if not queues[k] or n >= NP:
                        continue
                    what, i, rt = queues[k][0]
                    if what == "base":
                        if tick < BASE_TICK:
                            continue
                        c, half = i
                        if (rt, half) not in acc:
                            acc[(rt, half)] = sums.tile([P, N_COLS], F32, name="acc", tag="s%d%d" % (rt, half))
                        base_pass(rt, half, c)
                    else:
                        chunk, half, c = item_parts(i)
                        unit = ("r0", c // 2) if rt < 2 else ("t2", c // 4)
                        if i > tick - LAGW or quantised.get(unit, 99) >= tick:
                            continue
                        spline_passes((rt,), half, c)
                    if done[(rt, half)] == GROUP_PASSES:
                        to_close.append((rt, half))
                    queues[k] = queues[k][1:]
                    n += 1
                    moved = True
            pending = queues[0] + queues[1]
            n = 0
            while last and n < LASTMX:
                what, i = last[0]
                if what == "base":
                    if LAST_IN_WT:
                        if tick <= ITEMS:
                            break
                        acc[(3, i)] = psum.tile([P, N_COLS], F32, name="acc", tag="wt")
                    else:
                        if (i, 0) not in closed:
                            break
                        acc[(3, i)] = sums.tile([P, N_COLS], F32, name="acc", tag="s%d0" % i)
                    base_passes((3,), i)
                else:
                    c, half = i
                    unit = ("t3", c // 4)
                    if SPLIT_LAST and unit == units[-1]:
                        unit = (unit, c % 2)
                    if quantised.get(unit, 99) >= tick or quantised.get(("item", item_of[i]), 99) >= tick:
                        break
                    spline_passes((3,), half, c)
                    if done[(3, half)] == GROUP_PASSES:
                        to_close += [(3, half)]
                last = last[1:]
                n += 1
            tick += 1
